import numpy as np
import ml_dtypes


def mxq(x, axis, fmt="e4m3"):
    dtype, down = {"e4m3": (ml_dtypes.float8_e4m3fn, 7), "e5m2": (ml_dtypes.float8_e5m2, 14)}[fmt]
    v = np.moveaxis(np.asarray(x, np.float32).astype(ml_dtypes.bfloat16).astype(np.float64), axis, -1)
    blocks = v.reshape(v.shape[:-1] + (-1, 32))
    amax = np.abs(blocks).max(-1, keepdims=True)
    byte = np.maximum(np.where(amax > 0, np.frexp(amax)[1] - 1 + 127, 0) - down, 1)
    scale = np.exp2(byte - 127.0)
    codes = (blocks / scale).astype(np.float32).astype(dtype).astype(np.float64)
    return np.moveaxis((codes * scale).reshape(v.shape), -1, axis)


WIDE = False


def mx_kscale(k):
    if not WIDE:
        return np.ones(k)
    levels = np.array([10, -10, 5, -5, 0])
    a = np.random.permutation(np.resize(levels, k // 512 * 4)).reshape(k // 512, 4)
    idx = np.arange(k)
    return np.exp2(a[idx // 512, idx % 128 // 32])


BF16 = ml_dtypes.bfloat16


def bf(x):
    return np.asarray(x, np.float32).astype(BF16)


def f64(x):
    return np.asarray(x).astype(np.float64)


B, S, D, H, HD, C = 8, 1024, 1024, 1, 128, 2
DM = HD * C
DIFF = C - 1
EPS = 1e-9


def softmax(z):
    e = np.exp(z - z.max(-1, keepdims=True))
    return e / e.sum(-1, keepdims=True)


def setup_inputs():
    s = mx_kscale(D)
    a = np.sqrt(0.085 / (H * np.sqrt(HD)))
    return {"q_rot": bf(np.random.standard_normal((B, S, H, DM))),
            "k_rot": bf(np.random.standard_normal((B, S, H, DM))),
            "h_norm": bf(np.random.standard_normal((B, S, D)) * s),
            "wv": bf(np.random.standard_normal((H * HD, D)) / np.sqrt(D) / s[None, :]),
            "head_norm_w": bf(1.0 + 0.1 * np.random.standard_normal(HD)),
            "q1": bf(np.random.standard_normal((H, HD, DIFF)) * a),
            "q2": bf(np.random.standard_normal((H, HD, DIFF)) * a),
            "k1": bf(np.random.standard_normal((H, HD, DIFF)) * a),
            "k2": bf(np.random.standard_normal((H, HD, DIFF)) * a),
            "lam_init": bf(0.5 / H + 0.08 / np.sqrt(H) * np.random.standard_normal(H))}


def reference(q_rot, k_rot, h_norm, wv, head_norm_w, q1, q2, k1, k2, lam_init):
    lam = f64(lam_init)
    v = (mxq(f64(h_norm), 2, "e4m3") @ mxq(f64(wv), 1, "e4m3").T).reshape(B, S, H, HD)
    qc = f64(q_rot).reshape(B, S, H, C, HD).transpose(0, 2, 3, 1, 4)
    kc = f64(k_rot).reshape(B, S, H, C, HD).transpose(0, 2, 3, 4, 1)
    energy = qc @ kc
    mask = np.triu(np.ones((S, S), dtype=bool), 1)
    energy = np.where(mask, -np.inf, energy)
    scores = softmax(energy / np.sqrt(HD))
    base = np.exp(np.sum(f64(q1) * f64(k1), axis=-2)) - np.exp(np.sum(f64(q2) * f64(k2), axis=-2))
    scale = -(H * base[:, 0] + np.sum(lam))
    sc = scores[:, :, 0] + scores[:, :, 1] * scale[None, :, None, None]
    vv = v.transpose(0, 2, 1, 3)
    att = (mxq(sc, 3, "e4m3") @ mxq(vv, 2, "e4m3")).transpose(0, 2, 1, 3)
    att = att / np.sqrt(np.mean(att * att, axis=-1, keepdims=True) + EPS) * f64(head_norm_w)
    return att * (1.0 - lam[None, None, :, None])

@@ -1,0 +1,411 @@
+import math
+from contextlib import ExitStack
+
+import concourse.mybir as mybir
+from concourse.masks import make_identity
+
+F32 = mybir.dt.float32
+BF16 = mybir.dt.bfloat16
+U32 = mybir.dt.uint32
+U8 = mybir.dt.uint8
+FP8X4 = mybir.dt.float8_e4m3fn_x4
+ALU = mybir.AluOpType
+ACT = mybir.ActivationFunctionType
+AXIS = mybir.AxisListType
+
+B, S, D, HD, C = 8, 1024, 1024, 128, 2
+EPS = 1e-9
+P = 128
+TILES = S // P
+BANK = 512
+K_PASS = 512
+ITEMS = B * TILES
+GROUP = 4
+SM_SCALE = 1.0 / math.sqrt(HD)
+MASKED = -1.0e30
+
+FLOPS = 2 * B * S * D * HD + 2 * B * C * S * S * HD + 2 * B * S * S * HD
+
+
+def key_passes(it):
+    return (it * P) // K_PASS + 1
+
+
+def tile_attention_pb_t_kernel(
+    tc, q_rot, k_rot, h_norm, wv, head_norm_w, q1, q2, k1, k2, lam_init, out
+):
+    nc = tc.nc
+    with ExitStack() as ctx:
+        ctx.enter_context(tc.manual_schedule())
+        const = ctx.enter_context(tc.tile_pool(name="const", bufs=1))
+        raw = ctx.enter_context(tc.tile_pool(name="raw", bufs=2))
+        batch = ctx.enter_context(tc.tile_pool(name="batch", bufs=2))
+        stage = ctx.enter_context(tc.tile_pool(name="stage", bufs=3))
+        soft = ctx.enter_context(tc.tile_pool(name="soft", bufs=2))
+        stat = ctx.enter_context(tc.tile_pool(name="stat", bufs=4))
+        codes = ctx.enter_context(tc.tile_pool(name="codes", bufs=6))
+        psum_e = ctx.enter_context(tc.psum_pool(name="psum_e", bufs=4))
+        psum_in = ctx.enter_context(tc.psum_pool(name="psum_in", bufs=2))
+        psum_sc = ctx.enter_context(tc.psum_pool(name="psum_sc", bufs=1))
+        psum_att = ctx.enter_context(tc.psum_pool(name="psum_att", bufs=1))
+
+        h_raw, q_raw, k_raw = {}, {}, {}
+        h_grouped, h_codes, h_scales = {}, {}, {}
+        q_t, k_t = {}, {}
+        v_codes, v_scales = {}, {}
+        energy, neg_max, expo, sums, inv = {}, {}, {}, {}, {}
+        sc_grouped, sc_codes, sc_scales = {}, {}, {}
+        att, rstd = {}, {}
+
+        def load_h(b):
+            h_raw[b] = raw.tile([P, 4, 2 * D], BF16, name="h_raw")
+            h_view = h_norm[b].rearrange("(g p e) k -> p g (e k)", p=P, e=2)
+            for g in range(4):
+                nc.sync.dma_start(out=h_raw[b][:, g, :], in_=h_view[:, g, :])
+
+        def load_qk(b):
+            q_raw[b] = raw.tile([P, TILES, C * HD], BF16, name="q_raw")
+            nc.sync.dma_start(
+                out=q_raw[b][:], in_=q_rot[b, :, 0, :].rearrange("(t p) d -> p t d", p=P)
+            )
+            k_raw[b] = raw.tile([P, TILES, C * HD], BF16, name="k_raw")
+            nc.sync.dma_start(
+                out=k_raw[b][:], in_=k_rot[b, :, 0, :].rearrange("(t p) d -> p t d", p=P)
+            )
+
+        rows = const.tile([P, 6 * P], BF16, name="rows")
+        nc.vector.memset(rows[:], 0.0)
+        for i, vec in enumerate((q1, q2, k1, k2)):
+            nc.sync.dma_start(out=rows[0:1, i * P : (i + 1) * P], in_=vec.rearrange("h d o -> h (d o)"))
+        nc.sync.dma_start(out=rows[0:1, 4 * P : 5 * P], in_=head_norm_w.rearrange("(o d) -> o d", o=1))
+        nc.sync.dma_start(out=rows[0:1, 5 * P : 5 * P + 1], in_=lam_init.rearrange("(o d) -> o d", o=1))
+        wv_raw = const.tile([P, D], BF16, name="wv_raw")
+        nc.sync.dma_start(out=wv_raw[:], in_=wv)
+        load_qk(0)
+
+        ident_f32 = const.tile([P, P], F32, name="ident_f32")
+        make_identity(nc, ident_f32[:])
+        ident_bf = const.tile([P, P], BF16, name="ident_bf")
+        make_identity(nc, ident_bf[:])
+        mask_f32 = const.tile([P, P], F32, name="mask_f32")
+        nc.gpsimd.memset(mask_f32[:], 0.0)
+        nc.gpsimd.affine_select(
+            out=mask_f32[:],
+            in_=mask_f32[:],
+            compare_op=ALU.is_ge,
+            fill=MASKED,
+            base=0,
+            pattern=[[-1, P]],
+            channel_multiplier=1,
+        )
+        mask_bf = const.tile([P, P], BF16, name="mask_bf")
+        nc.vector.tensor_copy(out=mask_bf[:], in_=mask_f32[:])
+        neg_half = const.tile([P, GROUP], F32, name="neg_half")
+        nc.gpsimd.memset(neg_half[:], -0.5)
+        ones_bf = const.tile([P, P], BF16, name="ones_bf")
+        nc.vector.memset(ones_bf[:], 1.0)
+
+        sc_rows = []
+        for it in range(TILES):
+            sc_tile = const.tile([P, key_passes(it) * K_PASS], BF16, name="sc_rows%d" % it)
+            if (it + 1) * P < key_passes(it) * K_PASS:
+                nc.vector.memset(sc_tile[:, (it + 1) * P :], 0.0)
+            sc_rows.append(sc_tile)
+
+        def words_to_k_major(src_bf16, grouped):
+            words = src_bf16.bitcast(F32)
+            bank = psum_in.tile([P, 4, P], F32, name="word_bank", tag="tin")
+            for w in range(4):
+                nc.tensor.transpose(bank[:, w, :], words[:, w * P : (w + 1) * P], ident_f32[:])
+            nc.scalar.copy(
+                out=grouped[:].bitcast(F32), in_=bank[:].rearrange("p (g u) r -> p g r u", u=2)
+            )
+
+        wv_grouped = const.tile([P, 2, P, 4], BF16, name="wv_grouped", align_bytes=64)
+        words_to_k_major(wv_raw[:], wv_grouped)
+        wv_codes = const.tile([P, 2, P], U32, name="wv_codes", align_bytes=64)
+        wv_scales = const.tile([P, 2, P], U8, name="wv_scales", align_bytes=64)
+        nc.vector.quantize_mx(
+            out=wv_codes[:].rearrange("p g r -> p (g r)").bitcast(FP8X4),
+            scales=wv_scales[:].rearrange("p g r -> p (g r)"),
+            in_=wv_grouped[:].rearrange("p g r t -> p (g r t)"),
+        )
+
+        spread = const.tile([P, 6 * P], F32, name="spread")
+        bank_a = psum_in.tile([P, 4 * P], F32, name="bank_a", tag="tin")
+        nc.tensor.matmul(bank_a[:], lhsT=ones_bf[:], rhs=rows[:, : 4 * P], start=True, stop=True)
+        nc.vector.tensor_copy(out=spread[:, : 4 * P], in_=bank_a[:])
+        bank_b = psum_in.tile([P, 2 * P], F32, name="bank_b", tag="tin")
+        nc.tensor.matmul(bank_b[:], lhsT=ones_bf[:], rhs=rows[:, 4 * P :], start=True, stop=True)
+        nc.vector.tensor_copy(out=spread[:, 4 * P :], in_=bank_b[:])
+        lam = spread[:, 5 * P : 5 * P + 1]
+        products = const.tile([P, 2, P], F32, name="products")
+        nc.vector.tensor_tensor(
+            out=products[:].rearrange("p a d -> p (a d)"),
+            in0=spread[:, : 2 * P],
+            in1=spread[:, 2 * P : 4 * P],
+            op=ALU.mult,
+        )
+        dots = const.tile([P, 2], F32, name="dots")
+        nc.vector.tensor_reduce(out=dots[:], in_=products[:], axis=AXIS.X, op=ALU.add)
+        exp_dots = const.tile([P, 2], F32, name="exp_dots")
+        nc.scalar.activation(out=exp_dots[:], in_=dots[:], func=ACT.Exp)
+        scale = const.tile([P, 1], F32, name="scale")
+        nc.vector.tensor_tensor(out=scale[:], in0=exp_dots[:, 1:2], in1=exp_dots[:, 0:1], op=ALU.subtract)
+        nc.vector.tensor_tensor(out=scale[:], in0=scale[:], in1=lam, op=ALU.subtract)
+        one_minus_lam = const.tile([P, 1], F32, name="one_minus_lam")
+        nc.vector.tensor_scalar(
+            out=one_minus_lam[:], in0=lam, scalar1=-1.0, scalar2=1.0, op0=ALU.mult, op1=ALU.add
+        )
+        gain = const.tile([P, HD], F32, name="gain")
+        nc.vector.tensor_scalar(
+            out=gain[:], in0=spread[:, 4 * P : 5 * P], scalar1=one_minus_lam[:], scalar2=None, op0=ALU.mult
+        )
+
+        def transpose_h(m):
+            b, st = divmod(m, TILES)
+            g, e = divmod(st, 2)
+            h_grouped[m] = stage.tile([P, 2, P, 4], BF16, name="h_grouped", align_bytes=64)
+            words_to_k_major(h_raw[b][:, g, e * D : (e + 1) * D], h_grouped[m])
+
+        def quantise_h(m):
+            b, st = divmod(m, TILES)
+            if st == 0:
+                h_codes[b] = batch.tile([P, TILES, 2, P], U32, name="h_codes", align_bytes=64)
+                h_scales[b] = batch.tile([P, TILES, 2, P], U8, name="h_scales", align_bytes=64)
+            nc.vector.quantize_mx(
+                out=h_codes[b][:, st].rearrange("p g r -> p (g r)").bitcast(FP8X4),
+                scales=h_scales[b][:, st].rearrange("p g r -> p (g r)"),
+                in_=h_grouped[m][:].rearrange("p g r t -> p (g r t)"),
+            )
+
+        def project_v(vg):
+            b, kp = divmod(vg, 2)
+            v_bank = psum_in.tile([P, 4, HD], F32, name="v_bank", tag="tin")
+            for t in range(4):
+                st = 4 * kp + t
+                for g in range(2):
+                    nc.tensor.matmul_mx(
+                        out=v_bank[:, t, :],
+                        lhsT=h_codes[b][:, st, g, :].bitcast(FP8X4),
+                        lhsT_scale=h_scales[b][:, st, g, :],
+                        rhs=wv_codes[:, g, :].bitcast(FP8X4),
+                        rhs_scale=wv_scales[:, g, :],
+                        start=(g == 0),
+                        stop=(g == 1),
+                    )
+            v_grouped = stage.tile([P, HD, 4], BF16, name="v_grouped", align_bytes=64)
+            nc.scalar.copy(out=v_grouped[:], in_=v_bank[:].rearrange("p t d -> p d t"))
+            return v_grouped
+
+        def quantise_v(vg, v_grouped):
+            b, kp = divmod(vg, 2)
+            if kp == 0:
+                v_codes[b] = batch.tile([P, 2, HD], U32, name="v_codes", align_bytes=64)
+                v_scales[b] = batch.tile([P, 2, HD], U8, name="v_scales", align_bytes=64)
+            nc.vector.quantize_mx(
+                out=v_codes[b][:, kp, :].bitcast(FP8X4),
+                scales=v_scales[b][:, kp, :],
+                in_=v_grouped[:].rearrange("p d t -> p (d t)"),
+            )
+
+        def transpose_qk(b, piece, copy_out):
+            c, is_k = divmod(piece, 2)
+            if piece == 0:
+                q_t[b] = batch.tile([P, C, S], BF16, name="q_t")
+                k_t[b] = batch.tile([P, C, S], BF16, name="k_t")
+            src = k_raw[b] if is_k else q_raw[b]
+            dst = k_t[b] if is_k else q_t[b]
+            bank = psum_in.tile([P, TILES, P], BF16, name="qk_bank", tag="tin")
+            for t in range(TILES):
+                nc.tensor.transpose(bank[:, t, :], src[:, t, c * HD : (c + 1) * HD], ident_bf[:])
+            copy_out(out=dst[:, c, :], in_=bank[:].rearrange("p t r -> p (t r)"))
+
+        def energies(n):
+            b, it = divmod(n, TILES)
+            width = (it + 1) * P
+            energy[n] = []
+            for lo in range(0, width, BANK):
+                cols = min(BANK, width - lo)
+                for c in range(C):
+                    bank = psum_e.tile([P, BANK], F32, name="energy")
+                    has_diagonal = lo + cols == width
+                    nc.tensor.matmul(
+                        bank[:, :cols],
+                        lhsT=q_t[b][:, c, it * P : (it + 1) * P],
+                        rhs=k_t[b][:, c, lo : lo + cols],
+                        start=True,
+                        stop=not has_diagonal,
+                    )
+                    if has_diagonal:
+                        nc.tensor.matmul(
+                            bank[:, cols - P : cols], lhsT=ident_bf[:], rhs=mask_bf[:], start=False, stop=True
+                        )
+                    energy[n].append((c, lo, cols, bank))
+
+        def scale_and_max(n):
+            y = [soft.tile([P, S], F32, name="y%d" % c) for c in range(C)]
+            neg_max[n] = stat.tile([P, C, 2], F32, name="neg_max")
+            for c, lo, cols, bank in energy[n]:
+                chunk = lo // BANK
+                nc.vector.tensor_scalar(
+                    out=y[c][:, lo : lo + cols],
+                    in0=bank[:, :cols],
+                    scalar1=-SM_SCALE,
+                    scalar2=None if chunk == 0 else neg_max[n][:, c, chunk - 1 : chunk],
+                    op0=ALU.mult,
+                    op1=ALU.min,
+                    accum_out=neg_max[n][:, c, chunk : chunk + 1],
+                )
+            return y
+
+        def exponentials(n, y):
+            it = n % TILES
+            width = (it + 1) * P
+            last = (width - 1) // BANK
+            expo[n] = [soft.tile([P, S], F32, name="expo%d" % c, bufs=3) for c in range(C)]
+            sums[n] = stat.tile([P, C], F32, name="sums")
+            for c in range(C):
+                nc.scalar.activation(
+                    out=expo[n][c][:, :width],
+                    in_=y[c][:, :width],
+                    func=ACT.Exp,
+                    bias=neg_max[n][:, c, last : last + 1],
+                    scale=-1.0,
+                    accum_out=sums[n][:, c : c + 1],
+                )
+
+        def weigh_second(n):
+            width = (n % TILES + 1) * P
+            inv[n] = stat.tile([P, C], F32, name="inv")
+            nc.vector.reciprocal(out=inv[n][:], in_=sums[n][:])
+            nc.vector.tensor_scalar(
+                out=expo[n][1][:, :width],
+                in0=expo[n][1][:, :width],
+                scalar1=inv[n][:, 1:2],
+                scalar2=scale[:],
+                op0=ALU.mult,
+                op1=ALU.mult,
+            )
+
+        def combine(n):
+            it = n % TILES
+            width = (it + 1) * P
+            nc.vector.scalar_tensor_tensor(
+                out=sc_rows[it][:, :width],
+                in0=expo[n][0][:, :width],
+                scalar=inv[n][:, 0:1],
+                in1=expo[n][1][:, :width],
+                op0=ALU.mult,
+                op1=ALU.add,
+            )
+
+        def transpose_sc(n):
+            it = n % TILES
+            passes = key_passes(it)
+            words = sc_rows[it][:].bitcast(F32)
+            bank = psum_sc.tile([P, 4, P], F32, name="sc_bank")
+            for w in range(2 * passes):
+                nc.tensor.transpose(bank[:, w, :], words[:, w * P : (w + 1) * P], ident_f32[:])
+            sc_grouped[n] = stage.tile([P, 2, P, 4], BF16, name="sc_grouped", align_bytes=64)
+            nc.scalar.copy(
+                out=sc_grouped[n][:, :passes].bitcast(F32),
+                in_=bank[:, : 2 * passes, :].rearrange("p (g u) r -> p g r u", u=2),
+            )
+
+        def quantise_sc(n):
+            passes = key_passes(n % TILES)
+            sc_codes[n] = codes.tile([P, 2, P], U32, name="sc_codes", align_bytes=64)
+            sc_scales[n] = codes.tile([P, 2, P], U8, name="sc_scales", align_bytes=64)
+            nc.vector.quantize_mx(
+                out=sc_codes[n][:, :passes].rearrange("p g r -> p (g r)").bitcast(FP8X4),
+                scales=sc_scales[n][:, :passes].rearrange("p g r -> p (g r)"),
+                in_=sc_grouped[n][:, :passes].rearrange("p g r t -> p (g r t)"),
+            )
+
+        def attend(group):
+            b = (group * GROUP) // TILES
+            att[group] = psum_att.tile([P, GROUP, HD], F32, name="att")
+            for j in range(GROUP):
+                n = group * GROUP + j
+                passes = key_passes(n % TILES)
+                for kp in range(passes):
+                    nc.tensor.matmul_mx(
+                        out=att[group][:, j, :],
+                        lhsT=sc_codes[n][:, kp, :].bitcast(FP8X4),
+                        lhsT_scale=sc_scales[n][:, kp, :],
+                        rhs=v_codes[b][:, kp, :].bitcast(FP8X4),
+                        rhs_scale=v_scales[b][:, kp, :],
+                        start=(kp == 0),
+                        stop=(kp == passes - 1),
+                    )
+            squares = stage.tile([P, GROUP, HD], F32, name="squares")
+            sum_sq = stat.tile([P, GROUP], F32, name="sum_sq")
+            for j in range(GROUP):
+                nc.scalar.activation(
+                    out=squares[:, j, :], in_=att[group][:, j, :], func=ACT.Square, accum_out=sum_sq[:, j : j + 1]
+                )
+            mean_sq = stat.tile([P, GROUP], F32, name="mean_sq")
+            nc.gpsimd.tensor_scalar(
+                out=mean_sq[:], in0=sum_sq[:], scalar1=1.0 / HD, scalar2=EPS, op0=ALU.mult, op1=ALU.add
+            )
+            rstd[group] = stat.tile([P, GROUP], F32, name="rstd")
+            nc.gpsimd.tensor_tensor(out=rstd[group][:], in0=mean_sq[:], in1=neg_half[:], op=ALU.pow)
+
+        def finish(group):
+            b, half = divmod(group, TILES // GROUP)
+            result = stage.tile([P, GROUP, HD], F32, name="result")
+            for j in range(GROUP):
+                nc.vector.scalar_tensor_tensor(
+                    out=result[:, j, :],
+                    in0=att[group][:, j, :],
+                    scalar=rstd[group][:, j : j + 1],
+                    in1=gain[:],
+                    op0=ALU.mult,
+                    op1=ALU.mult,
+                )
+            first = half * GROUP * P
+            nc.sync.dma_start(
+                out=out[b, first : first + GROUP * P, 0, :].rearrange("(j p) d -> p j d", p=P), in_=result[:]
+            )
+
+        def is_item(n):
+            return 0 <= n < ITEMS
+
+        for s in range(-TILES, ITEMS + 9):
+            if s % TILES == 0:
+                if s // TILES + 2 < B:
+                    load_qk(s // TILES + 2)
+                if s // TILES + 1 < B:
+                    load_h(s // TILES + 1)
+
+            if is_item(s - 3):
+                transpose_sc(s - 3)
+            if is_item(s):
+                transpose_h(s)
+            qk_batch, qk_piece = divmod(s + 5, TILES)
+            if qk_piece < 4 and 0 <= qk_batch < B:
+                transpose_qk(qk_batch, qk_piece, nc.vector.tensor_copy if s < 0 else nc.scalar.copy)
+            if (s - 7) % GROUP == 0 and is_item(s - 7):
+                attend((s - 7) // GROUP)
+            v_grouped = None
+            if (s - 5) % 4 == 0 and is_item(s - 5):
+                v_grouped = project_v((s - 5) // 4)
+
+            if is_item(s):
+                y = scale_and_max(s)
+                exponentials(s, y)
+            if is_item(s + 1):
+                energies(s + 1)
+            if (s - 8) % GROUP == 0 and is_item(s - 8):
+                finish((s - 8) // GROUP)
+            if is_item(s - 2):
+                combine(s - 2)
+            if is_item(s - 3):
+                quantise_sc(s - 3)
+            if is_item(s - 1):
+                quantise_h(s - 1)
+            if v_grouped is not None:
+                quantise_v((s - 5) // 4, v_grouped)
+            if is_item(s - 1):
+                weigh_second(s - 1)

@@ -36,7 +36,6 @@ def tile_attention_pb_t_kernel(
 ):
     nc = tc.nc
     with ExitStack() as ctx:
-        ctx.enter_context(tc.manual_schedule())
         const = ctx.enter_context(tc.tile_pool(name="const", bufs=1))
         raw = ctx.enter_context(tc.tile_pool(name="raw", bufs=2))
         batch = ctx.enter_context(tc.tile_pool(name="batch", bufs=2))

@@ -230,9 +230,9 @@ def tile_attention_pb_t_kernel(
                     bank = psum_e.tile([P, BANK], F32, name="energy")
                     has_diagonal = lo + cols == width
                     nc.tensor.matmul(
-                        bank[:, :cols],
+                        bank[:],
                         lhsT=q_t[b][:, c, it * P : (it + 1) * P],
-                        rhs=k_t[b][:, c, lo : lo + cols],
+                        rhs=k_t[b][:, c, lo : lo + BANK],
                         start=True,
                         stop=not has_diagonal,
                     )

@@ -230,9 +230,9 @@ def tile_attention_pb_t_kernel(
                     bank = psum_e.tile([P, BANK], F32, name="energy")
                     has_diagonal = lo + cols == width
                     nc.tensor.matmul(
-                        bank[:],
+                        bank[:, :cols],
                         lhsT=q_t[b][:, c, it * P : (it + 1) * P],
-                        rhs=k_t[b][:, c, lo : lo + BANK],
+                        rhs=k_t[b][:, c, lo : lo + cols],
                         start=True,
                         stop=not has_diagonal,
                     )
@@ -278,7 +278,7 @@ def tile_attention_pb_t_kernel(
             width = (n % TILES + 1) * P
             inv[n] = stat.tile([P, C], F32, name="inv")
             nc.vector.reciprocal(out=inv[n][:], in_=sums[n][:])
-            nc.vector.tensor_scalar(
+            nc.gpsimd.tensor_scalar(
                 out=expo[n][1][:, :width],
                 in0=expo[n][1][:, :width],
                 scalar1=inv[n][:, 1:2],
@@ -307,7 +307,7 @@ def tile_attention_pb_t_kernel(
             for w in range(2 * passes):
                 nc.tensor.transpose(bank[:, w, :], words[:, w * P : (w + 1) * P], ident_f32[:])
             sc_grouped[n] = stage.tile([P, 2, P, 4], BF16, name="sc_grouped", align_bytes=64)
-            nc.scalar.copy(
+            nc.vector.tensor_copy(
                 out=sc_grouped[n][:, :passes].bitcast(F32),
                 in_=bank[:, : 2 * passes, :].rearrange("p (g u) r -> p g r u", u=2),
             )

@@ -22,6 +22,7 @@ K_PASS = 512
 ITEMS = B * TILES
 GROUP = 4
 SM_SCALE = 1.0 / math.sqrt(HD)
+LOG2_E = 1.0 / math.log(2.0)
 MASKED = -1.0e30
 
 FLOPS = 2 * B * S * D * HD + 2 * B * C * S * S * HD + 2 * B * S * S * HD
@@ -57,10 +58,12 @@ def tile_attention_pb_t_kernel(
         att, rstd = {}, {}
 
         def load_h(b):
-            h_raw[b] = raw.tile([P, 4, 2 * D], BF16, name="h_raw")
-            h_view = h_norm[b].rearrange("(g p e) k -> p g (e k)", p=P, e=2)
-            for g in range(4):
-                nc.sync.dma_start(out=h_raw[b][:, g, :], in_=h_view[:, g, :])
+            h_raw[b] = raw.tile([P, 2, 4 * D], BF16, name="h_raw")
+            h_view = h_norm[b].rearrange("(g p t) k -> p g (t k)", p=P, t=4)
+            for g in range(2):
+                for half in range(2):
+                    cols = slice(half * 2 * D, (half + 1) * 2 * D)
+                    nc.sync.dma_start(out=h_raw[b][:, g, cols], in_=h_view[:, g, cols])
 
         def load_qk(b):
             q_raw[b] = raw.tile([P, TILES, C * HD], BF16, name="q_raw")
@@ -147,8 +150,12 @@ def tile_attention_pb_t_kernel(
         )
         dots = const.tile([P, 2], F32, name="dots")
         nc.vector.tensor_reduce(out=dots[:], in_=products[:], axis=AXIS.X, op=ALU.add)
+        log2_exp = const.tile([P, 2], F32, name="log2_exp")
+        nc.vector.tensor_scalar(out=log2_exp[:], in0=dots[:], scalar1=LOG2_E, scalar2=None, op0=ALU.mult)
+        two = const.tile([P, 2], F32, name="two")
+        nc.gpsimd.memset(two[:], 2.0)
         exp_dots = const.tile([P, 2], F32, name="exp_dots")
-        nc.scalar.activation(out=exp_dots[:], in_=dots[:], func=ACT.Exp)
+        nc.gpsimd.tensor_tensor(out=exp_dots[:], in0=two[:], in1=log2_exp[:], op=ALU.pow)
         scale = const.tile([P, 1], F32, name="scale")
         nc.vector.tensor_tensor(out=scale[:], in0=exp_dots[:, 1:2], in1=exp_dots[:, 0:1], op=ALU.subtract)
         nc.vector.tensor_tensor(out=scale[:], in0=scale[:], in1=lam, op=ALU.subtract)
@@ -163,9 +170,9 @@ def tile_attention_pb_t_kernel(
 
         def transpose_h(m):
             b, st = divmod(m, TILES)
-            g, e = divmod(st, 2)
+            g, t = divmod(st, 4)
             h_grouped[m] = stage.tile([P, 2, P, 4], BF16, name="h_grouped", align_bytes=64)
-            words_to_k_major(h_raw[b][:, g, e * D : (e + 1) * D], h_grouped[m])
+            words_to_k_major(h_raw[b][:, g, t * D : (t + 1) * D], h_grouped[m])
 
         def quantise_h(m):
             b, st = divmod(m, TILES)
@@ -304,8 +311,11 @@ def tile_attention_pb_t_kernel(
             passes = key_passes(it)
             words = sc_rows[it][:].bitcast(F32)
             bank = psum_sc.tile([P, 4, P], F32, name="sc_bank")
-            for w in range(2 * passes):
-                nc.tensor.transpose(bank[:, w, :], words[:, w * P : (w + 1) * P], ident_f32[:])
+            for g in range(passes):
+                for u in range(2):
+                    nc.tensor.transpose(
+                        bank[:, 2 * g + u, :], words[:, 2 * P * g + u : 2 * P * (g + 1) : 2], ident_f32[:]
+                    )
             sc_grouped[n] = stage.tile([P, 2, P, 4], BF16, name="sc_grouped", align_bytes=64)
             nc.vector.tensor_copy(
                 out=sc_grouped[n][:, :passes].bitcast(F32),

@@ -21,6 +21,13 @@ BANK = 512
 K_PASS = 512
 ITEMS = B * TILES
 GROUP = 4
+PAIR = 2
+SC_EARLY = (0, 0, 0, 0, 0, 0, 0, 1)
+SC_ON_SCALAR = ()
+H_AHEAD = 1
+QK_FROM = 1
+V_AFTER, ATT_AT, FIN_AT = 3, 7, 9
+DIRECT_FROM = 5
 SM_SCALE = 1.0 / math.sqrt(HD)
 LOG2_E = 1.0 / math.log(2.0)
 MASKED = -1.0e30
@@ -37,6 +44,7 @@ def tile_attention_pb_t_kernel(
 ):
     nc = tc.nc
     with ExitStack() as ctx:
+        ctx.enter_context(tc.manual_schedule())
         const = ctx.enter_context(tc.tile_pool(name="const", bufs=1))
         raw = ctx.enter_context(tc.tile_pool(name="raw", bufs=2))
         batch = ctx.enter_context(tc.tile_pool(name="batch", bufs=2))
@@ -44,18 +52,18 @@ def tile_attention_pb_t_kernel(
         soft = ctx.enter_context(tc.tile_pool(name="soft", bufs=2))
         stat = ctx.enter_context(tc.tile_pool(name="stat", bufs=4))
         codes = ctx.enter_context(tc.tile_pool(name="codes", bufs=6))
-        psum_e = ctx.enter_context(tc.psum_pool(name="psum_e", bufs=4))
+        psum_e = ctx.enter_context(tc.psum_pool(name="psum_e", bufs=3))
+        psum_r = ctx.enter_context(tc.psum_pool(name="psum_r", bufs=2))
         psum_in = ctx.enter_context(tc.psum_pool(name="psum_in", bufs=2))
-        psum_sc = ctx.enter_context(tc.psum_pool(name="psum_sc", bufs=1))
         psum_att = ctx.enter_context(tc.psum_pool(name="psum_att", bufs=1))
 
         h_raw, q_raw, k_raw = {}, {}, {}
         h_grouped, h_codes, h_scales = {}, {}, {}
         q_t, k_t = {}, {}
         v_codes, v_scales = {}, {}
-        energy, neg_max, expo, sums, inv = {}, {}, {}, {}, {}
-        sc_grouped, sc_codes, sc_scales = {}, {}, {}
-        att, rstd = {}, {}
+        energy, rounded, neg_max, y, expo, sums, inv = {}, {}, {}, {}, {}, {}, {}
+        sc_bank, sc_grouped, sc_codes, sc_scales = {}, {}, {}, {}
+        att, sum_sq, rstd, part_sums = {}, {}, {}, {}
 
         def load_h(b):
             h_raw[b] = raw.tile([P, 2, 4 * D], BF16, name="h_raw")
@@ -78,15 +86,17 @@ def tile_attention_pb_t_kernel(
         rows = const.tile([P, 6 * P], BF16, name="rows")
         nc.vector.memset(rows[:], 0.0)
         for i, vec in enumerate((q1, q2, k1, k2)):
-            nc.sync.dma_start(out=rows[0:1, i * P : (i + 1) * P], in_=vec.rearrange("h d o -> h (d o)"))
-        nc.sync.dma_start(out=rows[0:1, 4 * P : 5 * P], in_=head_norm_w.rearrange("(o d) -> o d", o=1))
-        nc.sync.dma_start(out=rows[0:1, 5 * P : 5 * P + 1], in_=lam_init.rearrange("(o d) -> o d", o=1))
+            nc.scalar.dma_start(out=rows[0:1, i * P : (i + 1) * P], in_=vec.rearrange("h d o -> h (d o)"))
+        nc.scalar.dma_start(out=rows[0:1, 4 * P : 5 * P], in_=head_norm_w.rearrange("(o d) -> o d", o=1))
+        nc.scalar.dma_start(out=rows[0:1, 5 * P : 5 * P + 1], in_=lam_init.rearrange("(o d) -> o d", o=1))
+        load_qk(0)
         wv_raw = const.tile([P, D], BF16, name="wv_raw")
         nc.sync.dma_start(out=wv_raw[:], in_=wv)
-        load_qk(0)
 
-        ident_f32 = const.tile([P, P], F32, name="ident_f32")
-        make_identity(nc, ident_f32[:])
+        ones_bf = const.tile([P, P], BF16, name="ones_bf")
+        nc.vector.memset(ones_bf[:], 1.0)
+        two = const.tile([P, 2], F32, name="two")
+        nc.vector.memset(two[:], 2.0)
         ident_bf = const.tile([P, P], BF16, name="ident_bf")
         make_identity(nc, ident_bf[:])
         mask_f32 = const.tile([P, P], F32, name="mask_f32")
@@ -102,10 +112,10 @@ def tile_attention_pb_t_kernel(
         )
         mask_bf = const.tile([P, P], BF16, name="mask_bf")
         nc.vector.tensor_copy(out=mask_bf[:], in_=mask_f32[:])
+        ident_f32 = const.tile([P, P], F32, name="ident_f32")
+        make_identity(nc, ident_f32[:])
         neg_half = const.tile([P, GROUP], F32, name="neg_half")
         nc.gpsimd.memset(neg_half[:], -0.5)
-        ones_bf = const.tile([P, P], BF16, name="ones_bf")
-        nc.vector.memset(ones_bf[:], 1.0)
 
         sc_rows = []
         for it in range(TILES):
@@ -113,25 +123,6 @@ def tile_attention_pb_t_kernel(
             if (it + 1) * P < key_passes(it) * K_PASS:
                 nc.vector.memset(sc_tile[:, (it + 1) * P :], 0.0)
             sc_rows.append(sc_tile)
-
-        def words_to_k_major(src_bf16, grouped):
-            words = src_bf16.bitcast(F32)
-            bank = psum_in.tile([P, 4, P], F32, name="word_bank", tag="tin")
-            for w in range(4):
-                nc.tensor.transpose(bank[:, w, :], words[:, w * P : (w + 1) * P], ident_f32[:])
-            nc.scalar.copy(
-                out=grouped[:].bitcast(F32), in_=bank[:].rearrange("p (g u) r -> p g r u", u=2)
-            )
-
-        wv_grouped = const.tile([P, 2, P, 4], BF16, name="wv_grouped", align_bytes=64)
-        words_to_k_major(wv_raw[:], wv_grouped)
-        wv_codes = const.tile([P, 2, P], U32, name="wv_codes", align_bytes=64)
-        wv_scales = const.tile([P, 2, P], U8, name="wv_scales", align_bytes=64)
-        nc.vector.quantize_mx(
-            out=wv_codes[:].rearrange("p g r -> p (g r)").bitcast(FP8X4),
-            scales=wv_scales[:].rearrange("p g r -> p (g r)"),
-            in_=wv_grouped[:].rearrange("p g r t -> p (g r t)"),
-        )
 
         spread = const.tile([P, 6 * P], F32, name="spread")
         bank_a = psum_in.tile([P, 4 * P], F32, name="bank_a", tag="tin")
@@ -148,41 +139,61 @@ def tile_attention_pb_t_kernel(
             in1=spread[:, 2 * P : 4 * P],
             op=ALU.mult,
         )
-        dots = const.tile([P, 2], F32, name="dots")
-        nc.vector.tensor_reduce(out=dots[:], in_=products[:], axis=AXIS.X, op=ALU.add)
-        log2_exp = const.tile([P, 2], F32, name="log2_exp")
-        nc.vector.tensor_scalar(out=log2_exp[:], in0=dots[:], scalar1=LOG2_E, scalar2=None, op0=ALU.mult)
-        two = const.tile([P, 2], F32, name="two")
-        nc.gpsimd.memset(two[:], 2.0)
-        exp_dots = const.tile([P, 2], F32, name="exp_dots")
-        nc.gpsimd.tensor_tensor(out=exp_dots[:], in0=two[:], in1=log2_exp[:], op=ALU.pow)
-        scale = const.tile([P, 1], F32, name="scale")
-        nc.vector.tensor_tensor(out=scale[:], in0=exp_dots[:, 1:2], in1=exp_dots[:, 0:1], op=ALU.subtract)
-        nc.vector.tensor_tensor(out=scale[:], in0=scale[:], in1=lam, op=ALU.subtract)
         one_minus_lam = const.tile([P, 1], F32, name="one_minus_lam")
         nc.vector.tensor_scalar(
             out=one_minus_lam[:], in0=lam, scalar1=-1.0, scalar2=1.0, op0=ALU.mult, op1=ALU.add
         )
+        dots = const.tile([P, 2], F32, name="dots")
+        nc.vector.tensor_reduce(out=dots[:], in_=products[:], axis=AXIS.X, op=ALU.add)
         gain = const.tile([P, HD], F32, name="gain")
         nc.vector.tensor_scalar(
             out=gain[:], in0=spread[:, 4 * P : 5 * P], scalar1=one_minus_lam[:], scalar2=None, op0=ALU.mult
         )
+        log2_exp = const.tile([P, 2], F32, name="log2_exp")
+        nc.vector.tensor_scalar(out=log2_exp[:], in0=dots[:], scalar1=LOG2_E, scalar2=None, op0=ALU.mult)
+        exp_dots = const.tile([P, 2], F32, name="exp_dots")
+        nc.gpsimd.tensor_tensor(out=exp_dots[:], in0=two[:], in1=log2_exp[:], op=ALU.pow)
+        scale = const.tile([P, 1], F32, name="scale")
+        nc.gpsimd.tensor_tensor(out=scale[:], in0=exp_dots[:, 1:2], in1=exp_dots[:, 0:1], op=ALU.subtract)
+        nc.gpsimd.tensor_tensor(out=scale[:], in0=scale[:], in1=lam, op=ALU.subtract)
+
+        def words_to_k_major(src_bf16, grouped):
+            words = src_bf16.bitcast(F32)
+            bank = psum_in.tile([P, 4, P], F32, name="word_bank", tag="tin")
+            for w in range(4):
+                nc.tensor.transpose(bank[:, w, :], words[:, w * P : (w + 1) * P], ident_f32[:])
+            nc.scalar.copy(
+                out=grouped.bitcast(F32), in_=bank[:].rearrange("p (g u) r -> p g r u", u=2)
+            )
+
+        wv_grouped = const.tile([P, 2, P, 4], BF16, name="wv_grouped", align_bytes=64)
+        wv_codes = const.tile([P, 2, P], U32, name="wv_codes", align_bytes=64)
+        wv_scales = const.tile([P, 2, P], U8, name="wv_scales", align_bytes=64)
+
+        def quantise_wv():
+            nc.vector.quantize_mx(
+                out=wv_codes[:].rearrange("p g r -> p (g r)").bitcast(FP8X4),
+                scales=wv_scales[:].rearrange("p g r -> p (g r)"),
+                in_=wv_grouped[:].rearrange("p g r t -> p (g r t)"),
+            )
 
         def transpose_h(m):
             b, st = divmod(m, TILES)
             g, t = divmod(st, 4)
-            h_grouped[m] = stage.tile([P, 2, P, 4], BF16, name="h_grouped", align_bytes=64)
-            words_to_k_major(h_raw[b][:, g, t * D : (t + 1) * D], h_grouped[m])
+            if m % PAIR == 0:
+                h_grouped[m // PAIR] = stage.tile([P, PAIR, 2, P, 4], BF16, name="h_grouped", align_bytes=64)
+            words_to_k_major(h_raw[b][:, g, t * D : (t + 1) * D], h_grouped[m // PAIR][:, m % PAIR])
 
-        def quantise_h(m):
-            b, st = divmod(m, TILES)
-            if st == 0:
+        def quantise_h(pair):
+            b, half = divmod(pair, TILES // PAIR)
+            st = half * PAIR
+            if half == 0:
                 h_codes[b] = batch.tile([P, TILES, 2, P], U32, name="h_codes", align_bytes=64)
                 h_scales[b] = batch.tile([P, TILES, 2, P], U8, name="h_scales", align_bytes=64)
             nc.vector.quantize_mx(
-                out=h_codes[b][:, st].rearrange("p g r -> p (g r)").bitcast(FP8X4),
-                scales=h_scales[b][:, st].rearrange("p g r -> p (g r)"),
-                in_=h_grouped[m][:].rearrange("p g r t -> p (g r t)"),
+                out=h_codes[b][:, st : st + PAIR].rearrange("p i g r -> p (i g r)").bitcast(FP8X4),
+                scales=h_scales[b][:, st : st + PAIR].rearrange("p i g r -> p (i g r)"),
+                in_=h_grouped[pair][:].rearrange("p i g r t -> p (i g r t)"),
             )
 
         def project_v(vg):
@@ -200,6 +211,9 @@ def tile_attention_pb_t_kernel(
                         start=(g == 0),
                         stop=(g == 1),
                     )
+            return v_bank
+
+        def copy_v(v_bank):
             v_grouped = stage.tile([P, HD, 4], BF16, name="v_grouped", align_bytes=64)
             nc.scalar.copy(out=v_grouped[:], in_=v_bank[:].rearrange("p t d -> p d t"))
             return v_grouped
@@ -216,7 +230,7 @@ def tile_attention_pb_t_kernel(
             )
 
         def transpose_qk(b, piece, copy_out):
-            c, is_k = divmod(piece, 2)
+            c, is_k = 1 - piece // 2, piece % 2
             if piece == 0:
                 q_t[b] = batch.tile([P, C, S], BF16, name="q_t")
                 k_t[b] = batch.tile([P, C, S], BF16, name="k_t")
@@ -227,67 +241,111 @@ def tile_attention_pb_t_kernel(
                 nc.tensor.transpose(bank[:, t, :], src[:, t, c * HD : (c + 1) * HD], ident_bf[:])
             copy_out(out=dst[:, c, :], in_=bank[:].rearrange("p t r -> p (t r)"))
 
-        def energies(n):
-            b, it = divmod(n, TILES)
-            width = (it + 1) * P
-            energy[n] = []
-            for lo in range(0, width, BANK):
-                cols = min(BANK, width - lo)
-                for c in range(C):
-                    bank = psum_e.tile([P, BANK], F32, name="energy")
-                    has_diagonal = lo + cols == width
-                    nc.tensor.matmul(
-                        bank[:, :cols],
-                        lhsT=q_t[b][:, c, it * P : (it + 1) * P],
-                        rhs=k_t[b][:, c, lo : lo + cols],
-                        start=True,
-                        stop=not has_diagonal,
-                    )
-                    if has_diagonal:
-                        nc.tensor.matmul(
-                            bank[:, cols - P : cols], lhsT=ident_bf[:], rhs=mask_bf[:], start=False, stop=True
-                        )
-                    energy[n].append((c, lo, cols, bank))
+        def where(n):
+            return divmod(n, TILES)
 
-        def scale_and_max(n):
-            y = [soft.tile([P, S], F32, name="y%d" % c) for c in range(C)]
-            neg_max[n] = stat.tile([P, C, 2], F32, name="neg_max")
-            for c, lo, cols, bank in energy[n]:
-                chunk = lo // BANK
+        def is_item(n):
+            return 0 <= n < ITEMS
+
+        def is_direct(n):
+            return where(n)[1] >= DIRECT_FROM
+
+        def key_runs(n):
+            width = (where(n)[1] + 1) * P
+            return [(lo, min(BANK, width - lo)) for lo in range(0, width, BANK)]
+
+        def multiply_qk(n, c, lo, cols, dst):
+            b, it = where(n)
+            has_diagonal = lo + cols == (it + 1) * P
+            nc.tensor.matmul(
+                dst,
+                lhsT=q_t[b][:, c, it * P : (it + 1) * P],
+                rhs=k_t[b][:, c, lo : lo + cols],
+                start=True,
+                stop=not has_diagonal,
+            )
+            if has_diagonal:
+                nc.tensor.matmul(dst[:, cols - P :], lhsT=ident_bf[:], rhs=mask_bf[:], start=False, stop=True)
+
+        def rounded_energies(n, c):
+            rounded[n, c] = psum_r.tile([P, S], BF16, name="rounded")
+            for lo, cols in key_runs(n):
+                multiply_qk(n, c, lo, cols, rounded[n, c][:, lo : lo + cols])
+
+        def energies(n, c):
+            for lo, cols in key_runs(n):
+                bank = psum_e.tile([P, BANK], F32, name="energy")
+                energy[n, c, lo] = bank[:, :cols]
+                multiply_qk(n, c, lo, cols, energy[n, c, lo])
+
+        def row_max(n, c):
+            width = (where(n)[1] + 1) * P
+            neg_max[n, c] = stat.tile([P, 1], F32, name="neg_max%d" % c)
+            unused = soft.tile([P, S], BF16, name="unused")
+            nc.vector.tensor_scalar(
+                out=unused[:, :width],
+                in0=rounded[n, c][:, :width],
+                scalar1=-SM_SCALE,
+                scalar2=None,
+                op0=ALU.mult,
+                op1=ALU.min,
+                accum_out=neg_max[n, c][:],
+            )
+
+        def scale_and_max(n, c):
+            y[n, c] = soft.tile([P, DIRECT_FROM * P], F32, name="y%d" % c)
+            last = None
+            for lo, cols in key_runs(n):
+                neg_max[n, c] = stat.tile([P, 1], F32, name="neg_max%d" % c)
                 nc.vector.tensor_scalar(
-                    out=y[c][:, lo : lo + cols],
-                    in0=bank[:, :cols],
+                    out=y[n, c][:, lo : lo + cols],
+                    in0=energy[n, c, lo],
                     scalar1=-SM_SCALE,
-                    scalar2=None if chunk == 0 else neg_max[n][:, c, chunk - 1 : chunk],
+                    scalar2=last,
                     op0=ALU.mult,
                     op1=ALU.min,
-                    accum_out=neg_max[n][:, c, chunk : chunk + 1],
+                    accum_out=neg_max[n, c][:],
                 )
-            return y
+                last = neg_max[n, c][:]
 
-        def exponentials(n, y):
-            it = n % TILES
-            width = (it + 1) * P
-            last = (width - 1) // BANK
-            expo[n] = [soft.tile([P, S], F32, name="expo%d" % c, bufs=3) for c in range(C)]
-            sums[n] = stat.tile([P, C], F32, name="sums")
-            for c in range(C):
+        def exponentials(n, c):
+            width = (where(n)[1] + 1) * P
+            expo[n, c] = soft.tile([P, S], F32, name="expo%d" % c, bufs=3)
+            if c == 1:
+                sums[n] = stat.tile([P, C], F32, name="sums")
+                if is_direct(n):
+                    part_sums[n] = stat.tile([P, 2, C], F32, name="part")
+            if is_direct(n):
+                for lo, cols in key_runs(n):
+                    nc.scalar.activation(
+                        out=expo[n, c][:, lo : lo + cols],
+                        in_=energy[n, c, lo],
+                        func=ACT.Exp,
+                        bias=neg_max[n, c][:],
+                        scale=SM_SCALE,
+                        accum_out=part_sums[n][:, lo // BANK, c : c + 1],
+                    )
+            else:
                 nc.scalar.activation(
-                    out=expo[n][c][:, :width],
-                    in_=y[c][:, :width],
+                    out=expo[n, c][:, :width],
+                    in_=y[n, c][:, :width],
                     func=ACT.Exp,
-                    bias=neg_max[n][:, c, last : last + 1],
+                    bias=neg_max[n, c][:],
                     scale=-1.0,
                     accum_out=sums[n][:, c : c + 1],
                 )
 
+        def add_part_sums(n):
+            part = part_sums[n]
+            nc.gpsimd.tensor_tensor(out=sums[n][:], in0=part[:, 0, :], in1=part[:, 1, :], op=ALU.add)
+
         def weigh_second(n):
-            width = (n % TILES + 1) * P
+            width = (where(n)[1] + 1) * P
             inv[n] = stat.tile([P, C], F32, name="inv")
             nc.vector.reciprocal(out=inv[n][:], in_=sums[n][:])
             nc.gpsimd.tensor_scalar(
-                out=expo[n][1][:, :width],
-                in0=expo[n][1][:, :width],
+                out=expo[n, 1][:, :width],
+                in0=expo[n, 1][:, :width],
                 scalar1=inv[n][:, 1:2],
                 scalar2=scale[:],
                 op0=ALU.mult,
@@ -295,41 +353,60 @@ def tile_attention_pb_t_kernel(
             )
 
         def combine(n):
-            it = n % TILES
+            b, it = where(n)
             width = (it + 1) * P
             nc.vector.scalar_tensor_tensor(
                 out=sc_rows[it][:, :width],
-                in0=expo[n][0][:, :width],
+                in0=expo[n, 0][:, :width],
                 scalar=inv[n][:, 0:1],
-                in1=expo[n][1][:, :width],
+                in1=expo[n, 1][:, :width],
                 op0=ALU.mult,
                 op1=ALU.add,
             )
 
+        def sc_units(n):
+            if key_passes(where(n)[1]) == 2:
+                return [n]
+            return [n - 1, n] if n % PAIR == 1 else []
+
         def transpose_sc(n):
-            it = n % TILES
-            passes = key_passes(it)
-            words = sc_rows[it][:].bitcast(F32)
-            bank = psum_sc.tile([P, 4, P], F32, name="sc_bank")
-            for g in range(passes):
-                for u in range(2):
-                    nc.tensor.transpose(
-                        bank[:, 2 * g + u, :], words[:, 2 * P * g + u : 2 * P * (g + 1) : 2], ident_f32[:]
-                    )
-            sc_grouped[n] = stage.tile([P, 2, P, 4], BF16, name="sc_grouped", align_bytes=64)
-            nc.vector.tensor_copy(
-                out=sc_grouped[n][:, :passes].bitcast(F32),
-                in_=bank[:, : 2 * passes, :].rearrange("p (g u) r -> p g r u", u=2),
+            units = sc_units(n)
+            if not units:
+                return
+            sc_bank[n] = psum_in.tile([P, 4, P], F32, name="sc_bank", tag="tin")
+            slot = 0
+            for m in units:
+                words = sc_rows[where(m)[1]][:].bitcast(F32)
+                for g in range(key_passes(where(m)[1])):
+                    for u in range(2):
+                        nc.tensor.transpose(
+                            sc_bank[n][:, slot, :], words[:, 2 * P * g + u : 2 * P * (g + 1) : 2], ident_f32[:]
+                        )
+                        slot += 1
+
+        def copy_sc(n):
+            units = sc_units(n)
+            if not units:
+                return
+            passes = key_passes(where(n)[1])
+            pair = n // PAIR
+            if units[0] % PAIR == 0:
+                sc_grouped[pair] = stage.tile([P, PAIR * 2, P, 4], BF16, name="sc_grouped", align_bytes=64)
+            first = (units[0] % PAIR) * passes
+            copy_out = nc.scalar.copy if where(n)[1] in SC_ON_SCALAR else nc.vector.tensor_copy
+            copy_out(
+                out=sc_grouped[pair][:, first : first + 2].bitcast(F32),
+                in_=sc_bank[n][:].rearrange("p (g u) r -> p g r u", u=2),
             )
 
-        def quantise_sc(n):
-            passes = key_passes(n % TILES)
-            sc_codes[n] = codes.tile([P, 2, P], U32, name="sc_codes", align_bytes=64)
-            sc_scales[n] = codes.tile([P, 2, P], U8, name="sc_scales", align_bytes=64)
+        def quantise_sc(pair):
+            blocks = PAIR * key_passes(where(pair * PAIR)[1])
+            sc_codes[pair] = codes.tile([P, PAIR * 2, P], U32, name="sc_codes", align_bytes=64)
+            sc_scales[pair] = codes.tile([P, PAIR * 2, P], U8, name="sc_scales", align_bytes=64)
             nc.vector.quantize_mx(
-                out=sc_codes[n][:, :passes].rearrange("p g r -> p (g r)").bitcast(FP8X4),
-                scales=sc_scales[n][:, :passes].rearrange("p g r -> p (g r)"),
-                in_=sc_grouped[n][:, :passes].rearrange("p g r t -> p (g r t)"),
+                out=sc_codes[pair][:, :blocks].rearrange("p g r -> p (g r)").bitcast(FP8X4),
+                scales=sc_scales[pair][:, :blocks].rearrange("p g r -> p (g r)"),
+                in_=sc_grouped[pair][:, :blocks].rearrange("p g r t -> p (g r t)"),
             )
 
         def attend(group):
@@ -337,26 +414,32 @@ def tile_attention_pb_t_kernel(
             att[group] = psum_att.tile([P, GROUP, HD], F32, name="att")
             for j in range(GROUP):
                 n = group * GROUP + j
-                passes = key_passes(n % TILES)
+                pair = n // PAIR
+                passes = key_passes(where(n)[1])
                 for kp in range(passes):
+                    block = (n % PAIR) * passes + kp
                     nc.tensor.matmul_mx(
                         out=att[group][:, j, :],
-                        lhsT=sc_codes[n][:, kp, :].bitcast(FP8X4),
-                        lhsT_scale=sc_scales[n][:, kp, :],
+                        lhsT=sc_codes[pair][:, block, :].bitcast(FP8X4),
+                        lhsT_scale=sc_scales[pair][:, block, :],
                         rhs=v_codes[b][:, kp, :].bitcast(FP8X4),
                         rhs_scale=v_scales[b][:, kp, :],
                         start=(kp == 0),
                         stop=(kp == passes - 1),
                     )
+
+        def square_sums(group):
             squares = stage.tile([P, GROUP, HD], F32, name="squares")
-            sum_sq = stat.tile([P, GROUP], F32, name="sum_sq")
+            sum_sq[group] = stat.tile([P, GROUP], F32, name="sum_sq")
             for j in range(GROUP):
                 nc.scalar.activation(
-                    out=squares[:, j, :], in_=att[group][:, j, :], func=ACT.Square, accum_out=sum_sq[:, j : j + 1]
+                    out=squares[:, j, :], in_=att[group][:, j, :], func=ACT.Square, accum_out=sum_sq[group][:, j : j + 1]
                 )
+
+        def row_rms(group):
             mean_sq = stat.tile([P, GROUP], F32, name="mean_sq")
             nc.gpsimd.tensor_scalar(
-                out=mean_sq[:], in0=sum_sq[:], scalar1=1.0 / HD, scalar2=EPS, op0=ALU.mult, op1=ALU.add
+                out=mean_sq[:], in0=sum_sq[group][:], scalar1=1.0 / HD, scalar2=EPS, op0=ALU.mult, op1=ALU.add
             )
             rstd[group] = stat.tile([P, GROUP], F32, name="rstd")
             nc.gpsimd.tensor_tensor(out=rstd[group][:], in0=mean_sq[:], in1=neg_half[:], op=ALU.pow)
@@ -366,55 +449,105 @@ def tile_attention_pb_t_kernel(
             result = stage.tile([P, GROUP, HD], F32, name="result")
             for j in range(GROUP):
                 nc.vector.scalar_tensor_tensor(
-                    out=result[:, j, :],
+                    out=result[:, where(group * GROUP + j)[1] % GROUP, :],
                     in0=att[group][:, j, :],
                     scalar=rstd[group][:, j : j + 1],
                     in1=gain[:],
                     op0=ALU.mult,
                     op1=ALU.mult,
                 )
-            first = half * GROUP * P
+            first = min(where(group * GROUP + j)[1] for j in range(GROUP)) * P
             nc.sync.dma_start(
                 out=out[b, first : first + GROUP * P, 0, :].rearrange("(j p) d -> p j d", p=P), in_=result[:]
             )
 
-        def is_item(n):
-            return 0 <= n < ITEMS
+        v_bank, v_grouped = {}, {}
 
-        for s in range(-TILES, ITEMS + 9):
-            if s % TILES == 0:
-                if s // TILES + 2 < B:
-                    load_qk(s // TILES + 2)
-                if s // TILES + 1 < B:
-                    load_h(s // TILES + 1)
+        def h_step(m):
+            return max(m // 2, m - H_AHEAD)
 
-            if is_item(s - 3):
-                transpose_sc(s - 3)
-            if is_item(s):
-                transpose_h(s)
-            qk_batch, qk_piece = divmod(s + 5, TILES)
+        def at(s, offset, period):
+            k, r = divmod(s - offset, period)
+            return k if r == 0 and k >= 0 else None
+
+        for s in range(-TILES, ITEMS + 12):
+            b, it = divmod(s, TILES)
+            if it == 0:
+                if b + 2 < B:
+                    load_qk(b + 2)
+                if b + 1 < B:
+                    load_h(b + 1)
+
+            live = is_item(s)
+            direct = live and is_direct(s)
+            if live:
+                if direct:
+                    row_max(s, 1)
+                    energies(s, 1)
+                else:
+                    scale_and_max(s, 1)
+                exponentials(s, 1)
+            if is_item(s - 3) and where(s - 3)[1] in SC_ON_SCALAR:
+                copy_sc(s - 3)
+            for m in range(B * TILES):
+                if h_step(m) == s:
+                    transpose_h(m)
+            qk_batch, qk_piece = divmod(s + TILES - QK_FROM, TILES)
             if qk_piece < 4 and 0 <= qk_batch < B:
-                transpose_qk(qk_batch, qk_piece, nc.vector.tensor_copy if s < 0 else nc.scalar.copy)
-            if (s - 7) % GROUP == 0 and is_item(s - 7):
-                attend((s - 7) // GROUP)
-            v_grouped = None
-            if (s - 5) % 4 == 0 and is_item(s - 5):
-                v_grouped = project_v((s - 5) // 4)
-
-            if is_item(s):
-                y = scale_and_max(s)
-                exponentials(s, y)
+                transpose_qk(qk_batch, qk_piece, nc.scalar.copy)
+            if s == 1:
+                words_to_k_major(wv_raw[:], wv_grouped[:])
+            if s == 3:
+                quantise_wv()
+            if is_item(s - 3) and where(s - 3)[1] not in SC_ON_SCALAR:
+                copy_sc(s - 3)
+            f = at(s, FIN_AT, GROUP)
+            if f is not None and f < ITEMS // GROUP:
+                finish(f)
             if is_item(s + 1):
-                energies(s + 1)
-            if (s - 8) % GROUP == 0 and is_item(s - 8):
-                finish((s - 8) // GROUP)
+                if is_direct(s + 1):
+                    rounded_energies(s + 1, 1)
+                else:
+                    energies(s + 1, 1)
+            v_now = [vg for vg in range(2 * B) if h_step(4 * vg + 3) + V_AFTER == s]
+            for vg in v_now:
+                v_bank[vg] = project_v(vg)
+            group = at(s, ATT_AT, GROUP)
+            if group is not None and group < ITEMS // GROUP:
+                attend(group)
             if is_item(s - 2):
                 combine(s - 2)
-            if is_item(s - 3):
-                quantise_sc(s - 3)
-            if is_item(s - 1):
-                quantise_h(s - 1)
-            if v_grouped is not None:
-                quantise_v((s - 5) // 4, v_grouped)
+                if SC_EARLY[it]:
+                    transpose_sc(s - 2)
+            if live:
+                if direct:
+                    row_max(s, 0)
+                    energies(s, 0)
+                else:
+                    scale_and_max(s, 0)
+                exponentials(s, 0)
+            if is_item(s - 2) and not SC_EARLY[it]:
+                transpose_sc(s - 2)
+            if is_item(s + 1):
+                if is_direct(s + 1):
+                    rounded_energies(s + 1, 0)
+                else:
+                    energies(s + 1, 0)
+            for vg in v_now:
+                v_grouped[vg] = copy_v(v_bank[vg])
+            if group is not None and group < ITEMS // GROUP:
+                square_sums(group)
+            for pair in range(ITEMS // PAIR):
+                if h_step(PAIR * pair + 1) + 1 == s:
+                    quantise_h(pair)
+            for vg in range(2 * B):
+                if h_step(4 * vg + 3) + V_AFTER + 1 == s:
+                    quantise_v(vg, v_grouped[vg])
+            if s % PAIR == 0 and is_item(s - 3):
+                quantise_sc((s - 3) // PAIR)
             if is_item(s - 1):
                 weigh_second(s - 1)
+            if direct:
+                add_part_sums(s)
+            if group is not None and group < ITEMS // GROUP:
+                row_rms(group)

@@ -22,7 +22,6 @@ K_PASS = 512
 ITEMS = B * TILES
 GROUP = 4
 PAIR = 2
-SC_EARLY = (0, 0, 0, 0, 0, 0, 0, 1)
 SC_ON_SCALAR = ()
 H_AHEAD = 1
 QK_FROM = 1
@@ -515,10 +514,6 @@ def tile_attention_pb_t_kernel(
             group = at(s, ATT_AT, GROUP)
             if group is not None and group < ITEMS // GROUP:
                 attend(group)
-            if is_item(s - 2):
-                combine(s - 2)
-                if SC_EARLY[it]:
-                    transpose_sc(s - 2)
             if live:
                 if direct:
                     row_max(s, 0)
@@ -526,7 +521,8 @@ def tile_attention_pb_t_kernel(
                 else:
                     scale_and_max(s, 0)
                 exponentials(s, 0)
-            if is_item(s - 2) and not SC_EARLY[it]:
+            if is_item(s - 2):
+                combine(s - 2)
                 transpose_sc(s - 2)
             if is_item(s + 1):
                 if is_direct(s + 1):

@@ -23,9 +23,12 @@ ITEMS = B * TILES
 GROUP = 4
 PAIR = 2
 SC_ON_SCALAR = ()
-H_AHEAD = 1
-QK_FROM = 1
-V_AFTER, ATT_AT, FIN_AT = 3, 7, 9
+W_ON_VECTOR = ()
+EXPO_BUFS = 3
+H_LEAD, V_AFTER, QV_AFTER, WV_AT = 1, 2, 1, 0
+R_LAG, CB_LAG, T_LAG, CS_LAG, QS_LAG, ATT_LAG, F_LAG = 1, 2, 2, 3, 3, 5, 6
+TAIL_ORDER = """Ma Mw1 Mw0 Ew1 Ew0a Xa1 Xa0 Xw1 Ew0b Xw0 PS R W CSw CSa F Vt At Vc Sq RR CBw CBa Tw Ta QV QH QSw QSa"""
+ORDER = """Ma Mw1 Mw0 Ew1 Ew0a Xa1 Xa0 Xw1 Lw1 Ew0b Lw0 CSw CSa F Xw0 H0t H1t La1 QKt La0 H0c H1c QKc Vt At Vc Sq CBw CBa Tw Ta Ly QH QV QSw QSa R W PS RR WV"""
 DIRECT_FROM = 5
 SM_SCALE = 1.0 / math.sqrt(HD)
 LOG2_E = 1.0 / math.log(2.0)
@@ -53,10 +56,10 @@ def tile_attention_pb_t_kernel(
         codes = ctx.enter_context(tc.tile_pool(name="codes", bufs=6))
         psum_e = ctx.enter_context(tc.psum_pool(name="psum_e", bufs=3))
         psum_r = ctx.enter_context(tc.psum_pool(name="psum_r", bufs=2))
-        psum_in = ctx.enter_context(tc.psum_pool(name="psum_in", bufs=2))
-        psum_att = ctx.enter_context(tc.psum_pool(name="psum_att", bufs=1))
+        psum_in = ctx.enter_context(tc.psum_pool(name="psum_in", bufs=3))
+        psum_sc = psum_in
 
-        h_raw, q_raw, k_raw = {}, {}, {}
+        h_raw, q_raw, k_raw, h_bank, qk_bank, v_bank, v_grouped = {}, {}, {}, {}, {}, {}, {}
         h_grouped, h_codes, h_scales = {}, {}, {}
         q_t, k_t = {}, {}
         v_codes, v_scales = {}, {}
@@ -156,11 +159,14 @@ def tile_attention_pb_t_kernel(
         nc.gpsimd.tensor_tensor(out=scale[:], in0=exp_dots[:, 1:2], in1=exp_dots[:, 0:1], op=ALU.subtract)
         nc.gpsimd.tensor_tensor(out=scale[:], in0=scale[:], in1=lam, op=ALU.subtract)
 
-        def words_to_k_major(src_bf16, grouped):
+        def transpose_words(src_bf16):
             words = src_bf16.bitcast(F32)
             bank = psum_in.tile([P, 4, P], F32, name="word_bank", tag="tin")
             for w in range(4):
                 nc.tensor.transpose(bank[:, w, :], words[:, w * P : (w + 1) * P], ident_f32[:])
+            return bank
+
+        def copy_words(bank, grouped):
             nc.scalar.copy(
                 out=grouped.bitcast(F32), in_=bank[:].rearrange("p (g u) r -> p g r u", u=2)
             )
@@ -181,7 +187,10 @@ def tile_attention_pb_t_kernel(
             g, t = divmod(st, 4)
             if m % PAIR == 0:
                 h_grouped[m // PAIR] = stage.tile([P, PAIR, 2, P, 4], BF16, name="h_grouped", align_bytes=64)
-            words_to_k_major(h_raw[b][:, g, t * D : (t + 1) * D], h_grouped[m // PAIR][:, m % PAIR])
+            h_bank[m] = transpose_words(h_raw[b][:, g, t * D : (t + 1) * D])
+
+        def copy_h(m):
+            copy_words(h_bank[m], h_grouped[m // PAIR][:, m % PAIR])
 
         def quantise_h(pair):
             b, half = divmod(pair, TILES // PAIR)
@@ -197,12 +206,12 @@ def tile_attention_pb_t_kernel(
 
         def project_v(vg):
             b, kp = divmod(vg, 2)
-            v_bank = psum_in.tile([P, 4, HD], F32, name="v_bank", tag="tin")
+            v_bank[vg] = psum_in.tile([P, 4, HD], F32, name="v_bank", tag="tin")
             for t in range(4):
                 st = 4 * kp + t
                 for g in range(2):
                     nc.tensor.matmul_mx(
-                        out=v_bank[:, t, :],
+                        out=v_bank[vg][:, t, :],
                         lhsT=h_codes[b][:, st, g, :].bitcast(FP8X4),
                         lhsT_scale=h_scales[b][:, st, g, :],
                         rhs=wv_codes[:, g, :].bitcast(FP8X4),
@@ -210,14 +219,12 @@ def tile_attention_pb_t_kernel(
                         start=(g == 0),
                         stop=(g == 1),
                     )
-            return v_bank
 
-        def copy_v(v_bank):
-            v_grouped = stage.tile([P, HD, 4], BF16, name="v_grouped", align_bytes=64)
-            nc.scalar.copy(out=v_grouped[:], in_=v_bank[:].rearrange("p t d -> p d t"))
-            return v_grouped
+        def copy_v(vg):
+            v_grouped[vg] = stage.tile([P, HD, 4], BF16, name="v_grouped", align_bytes=64)
+            nc.scalar.copy(out=v_grouped[vg][:], in_=v_bank[vg][:].rearrange("p t d -> p d t"))
 
-        def quantise_v(vg, v_grouped):
+        def quantise_v(vg):
             b, kp = divmod(vg, 2)
             if kp == 0:
                 v_codes[b] = batch.tile([P, 2, HD], U32, name="v_codes", align_bytes=64)
@@ -225,26 +232,29 @@ def tile_attention_pb_t_kernel(
             nc.vector.quantize_mx(
                 out=v_codes[b][:, kp, :].bitcast(FP8X4),
                 scales=v_scales[b][:, kp, :],
-                in_=v_grouped[:].rearrange("p d t -> p (d t)"),
+                in_=v_grouped[vg][:].rearrange("p d t -> p (d t)"),
             )
 
-        def transpose_qk(b, piece, copy_out):
-            c, is_k = 1 - piece // 2, piece % 2
-            if piece == 0:
+        def transpose_qk(piece):
+            b, i = divmod(piece, 4)
+            c, is_k = 1 - i // 2, i % 2
+            if i == 0:
                 q_t[b] = batch.tile([P, C, S], BF16, name="q_t")
                 k_t[b] = batch.tile([P, C, S], BF16, name="k_t")
             src = k_raw[b] if is_k else q_raw[b]
-            dst = k_t[b] if is_k else q_t[b]
-            bank = psum_in.tile([P, TILES, P], BF16, name="qk_bank", tag="tin")
+            qk_bank[piece] = psum_in.tile([P, TILES, P], BF16, name="qk_bank", tag="tin")
             for t in range(TILES):
-                nc.tensor.transpose(bank[:, t, :], src[:, t, c * HD : (c + 1) * HD], ident_bf[:])
-            copy_out(out=dst[:, c, :], in_=bank[:].rearrange("p t r -> p (t r)"))
+                nc.tensor.transpose(qk_bank[piece][:, t, :], src[:, t, c * HD : (c + 1) * HD], ident_bf[:])
+
+        def copy_qk(piece, copy_out):
+            b, i = divmod(piece, 4)
+            c, is_k = 1 - i // 2, i % 2
+            dst = k_t[b] if is_k else q_t[b]
+            copy_out(out=dst[:, c, :], in_=qk_bank[piece][:].rearrange("p t r -> p (t r)"))
 
         def where(n):
-            return divmod(n, TILES)
-
-        def is_item(n):
-            return 0 <= n < ITEMS
+            b, i = divmod(n, TILES)
+            return b, (i // 2 if i % 2 == 0 else TILES - 1 - i // 2)
 
         def is_direct(n):
             return where(n)[1] >= DIRECT_FROM
@@ -271,8 +281,8 @@ def tile_attention_pb_t_kernel(
             for lo, cols in key_runs(n):
                 multiply_qk(n, c, lo, cols, rounded[n, c][:, lo : lo + cols])
 
-        def energies(n, c):
-            for lo, cols in key_runs(n):
+        def energies(n, c, runs=slice(None)):
+            for lo, cols in key_runs(n)[runs]:
                 bank = psum_e.tile([P, BANK], F32, name="energy")
                 energy[n, c, lo] = bank[:, :cols]
                 multiply_qk(n, c, lo, cols, energy[n, c, lo])
@@ -291,30 +301,32 @@ def tile_attention_pb_t_kernel(
                 accum_out=neg_max[n, c][:],
             )
 
-        def scale_and_max(n, c):
-            y[n, c] = soft.tile([P, DIRECT_FROM * P], F32, name="y%d" % c)
-            last = None
+        def scale_and_max(n, components):
+            for c in components:
+                y[n, c] = soft.tile([P, DIRECT_FROM * P], F32, name="y%d" % c)
             for lo, cols in key_runs(n):
-                neg_max[n, c] = stat.tile([P, 1], F32, name="neg_max%d" % c)
-                nc.vector.tensor_scalar(
-                    out=y[n, c][:, lo : lo + cols],
-                    in0=energy[n, c, lo],
-                    scalar1=-SM_SCALE,
-                    scalar2=last,
-                    op0=ALU.mult,
-                    op1=ALU.min,
-                    accum_out=neg_max[n, c][:],
-                )
-                last = neg_max[n, c][:]
+                for c in components:
+                    so_far = neg_max[n, c][:] if lo > 0 else None
+                    neg_max[n, c] = stat.tile([P, 1], F32, name="neg_max%d" % c)
+                    nc.vector.tensor_scalar(
+                        out=y[n, c][:, lo : lo + cols],
+                        in0=energy[n, c, lo],
+                        scalar1=-SM_SCALE,
+                        scalar2=so_far,
+                        op0=ALU.mult,
+                        op1=ALU.min,
+                        accum_out=neg_max[n, c][:],
+                    )
 
         def exponentials(n, c):
+            step, wide = divmod(n, 2)
             width = (where(n)[1] + 1) * P
-            expo[n, c] = soft.tile([P, S], F32, name="expo%d" % c, bufs=3)
-            if c == 1:
-                sums[n] = stat.tile([P, C], F32, name="sums")
-                if is_direct(n):
-                    part_sums[n] = stat.tile([P, 2, C], F32, name="part")
+            expo[n, c] = soft.tile([P, S if wide else BANK], F32, name="expo%d%d" % (wide, c), bufs=EXPO_BUFS)
+            if step not in sums:
+                sums[step] = stat.tile([P, 2, C], F32, name="sums")
             if is_direct(n):
+                if step not in part_sums:
+                    part_sums[step] = stat.tile([P, 2, C], F32, name="part")
                 for lo, cols in key_runs(n):
                     nc.scalar.activation(
                         out=expo[n, c][:, lo : lo + cols],
@@ -322,7 +334,7 @@ def tile_attention_pb_t_kernel(
                         func=ACT.Exp,
                         bias=neg_max[n, c][:],
                         scale=SM_SCALE,
-                        accum_out=part_sums[n][:, lo // BANK, c : c + 1],
+                        accum_out=part_sums[step][:, lo // BANK, c : c + 1],
                     )
             else:
                 nc.scalar.activation(
@@ -331,96 +343,86 @@ def tile_attention_pb_t_kernel(
                     func=ACT.Exp,
                     bias=neg_max[n, c][:],
                     scale=-1.0,
-                    accum_out=sums[n][:, c : c + 1],
+                    accum_out=sums[step][:, wide, c : c + 1],
                 )
 
-        def add_part_sums(n):
-            part = part_sums[n]
-            nc.gpsimd.tensor_tensor(out=sums[n][:], in0=part[:, 0, :], in1=part[:, 1, :], op=ALU.add)
+        def add_part_sums(step):
+            part = part_sums[step]
+            nc.gpsimd.tensor_tensor(out=sums[step][:, 1, :], in0=part[:, 0, :], in1=part[:, 1, :], op=ALU.add)
 
-        def weigh_second(n):
+        def invert_sums(step):
+            inv[step] = stat.tile([P, 2, C], F32, name="inv")
+            nc.vector.reciprocal(out=inv[step][:].rearrange("p i c -> p (i c)"), in_=sums[step][:].rearrange("p i c -> p (i c)"))
+
+        def weigh_second(n, engine):
+            step, wide = divmod(n, 2)
             width = (where(n)[1] + 1) * P
-            inv[n] = stat.tile([P, C], F32, name="inv")
-            nc.vector.reciprocal(out=inv[n][:], in_=sums[n][:])
-            nc.gpsimd.tensor_scalar(
+            engine.tensor_scalar(
                 out=expo[n, 1][:, :width],
                 in0=expo[n, 1][:, :width],
-                scalar1=inv[n][:, 1:2],
+                scalar1=inv[step][:, wide, 1:2],
                 scalar2=scale[:],
                 op0=ALU.mult,
                 op1=ALU.mult,
             )
 
         def combine(n):
+            step, wide = divmod(n, 2)
             b, it = where(n)
             width = (it + 1) * P
             nc.vector.scalar_tensor_tensor(
                 out=sc_rows[it][:, :width],
                 in0=expo[n, 0][:, :width],
-                scalar=inv[n][:, 0:1],
+                scalar=inv[step][:, wide, 0:1],
                 in1=expo[n, 1][:, :width],
                 op0=ALU.mult,
                 op1=ALU.add,
             )
 
-        def sc_units(n):
-            if key_passes(where(n)[1]) == 2:
-                return [n]
-            return [n - 1, n] if n % PAIR == 1 else []
-
-        def transpose_sc(n):
-            units = sc_units(n)
-            if not units:
-                return
-            sc_bank[n] = psum_in.tile([P, 4, P], F32, name="sc_bank", tag="tin")
+        def transpose_sc(items, key):
+            sc_bank[key] = psum_sc.tile([P, 4, P], F32, name="sc_bank", tag="tin")
             slot = 0
-            for m in units:
-                words = sc_rows[where(m)[1]][:].bitcast(F32)
-                for g in range(key_passes(where(m)[1])):
+            for n in items:
+                words = sc_rows[where(n)[1]][:].bitcast(F32)
+                for g in range(key_passes(where(n)[1])):
                     for u in range(2):
                         nc.tensor.transpose(
-                            sc_bank[n][:, slot, :], words[:, 2 * P * g + u : 2 * P * (g + 1) : 2], ident_f32[:]
+                            sc_bank[key][:, slot, :], words[:, 2 * P * g + u : 2 * P * (g + 1) : 2], ident_f32[:]
                         )
                         slot += 1
 
-        def copy_sc(n):
-            units = sc_units(n)
-            if not units:
-                return
-            passes = key_passes(where(n)[1])
-            pair = n // PAIR
-            if units[0] % PAIR == 0:
-                sc_grouped[pair] = stage.tile([P, PAIR * 2, P, 4], BF16, name="sc_grouped", align_bytes=64)
-            first = (units[0] % PAIR) * passes
-            copy_out = nc.scalar.copy if where(n)[1] in SC_ON_SCALAR else nc.vector.tensor_copy
+        def copy_sc(key, pair, first, copy_out):
+            wide = key % 2
+            if first == 0:
+                sc_grouped[pair, wide] = stage.tile([P, 4 if wide else 2, P, 4], BF16, name="sc_grouped%d" % wide, align_bytes=64)
             copy_out(
-                out=sc_grouped[pair][:, first : first + 2].bitcast(F32),
-                in_=sc_bank[n][:].rearrange("p (g u) r -> p g r u", u=2),
+                out=sc_grouped[pair, wide][:, first : first + 2].bitcast(F32),
+                in_=sc_bank[key][:].rearrange("p (g u) r -> p g r u", u=2),
             )
 
-        def quantise_sc(pair):
-            blocks = PAIR * key_passes(where(pair * PAIR)[1])
-            sc_codes[pair] = codes.tile([P, PAIR * 2, P], U32, name="sc_codes", align_bytes=64)
-            sc_scales[pair] = codes.tile([P, PAIR * 2, P], U8, name="sc_scales", align_bytes=64)
+        def quantise_sc(pair, wide):
+            blocks = 4 if wide else 2
+            sc_codes[pair, wide] = codes.tile([P, blocks, P], U32, name="sc_codes%d" % wide, align_bytes=64)
+            sc_scales[pair, wide] = codes.tile([P, blocks, P], U8, name="sc_scales%d" % wide, align_bytes=64)
             nc.vector.quantize_mx(
-                out=sc_codes[pair][:, :blocks].rearrange("p g r -> p (g r)").bitcast(FP8X4),
-                scales=sc_scales[pair][:, :blocks].rearrange("p g r -> p (g r)"),
-                in_=sc_grouped[pair][:, :blocks].rearrange("p g r t -> p (g r t)"),
+                out=sc_codes[pair, wide][:].rearrange("p g r -> p (g r)").bitcast(FP8X4),
+                scales=sc_scales[pair, wide][:].rearrange("p g r -> p (g r)"),
+                in_=sc_grouped[pair, wide][:].rearrange("p g r t -> p (g r t)"),
             )
 
         def attend(group):
-            b = (group * GROUP) // TILES
-            att[group] = psum_att.tile([P, GROUP, HD], F32, name="att")
+            b = group // 2
+            att[group] = psum_in.tile([P, GROUP, HD], F32, name="att", tag="tin")
             for j in range(GROUP):
                 n = group * GROUP + j
-                pair = n // PAIR
-                passes = key_passes(where(n)[1])
+                wide = n % 2
+                passes = 2 if wide else 1
                 for kp in range(passes):
-                    block = (n % PAIR) * passes + kp
+                    block = (j // 2) * passes + kp
                     nc.tensor.matmul_mx(
                         out=att[group][:, j, :],
-                        lhsT=sc_codes[pair][:, block, :].bitcast(FP8X4),
-                        lhsT_scale=sc_scales[pair][:, block, :],
+                        lhsT=sc_codes[group, wide][:, block, :].bitcast(FP8X4),
+                        lhsT_scale=sc_scales[group, wide][:, block, :],
                         rhs=v_codes[b][:, kp, :].bitcast(FP8X4),
                         rhs_scale=v_scales[b][:, kp, :],
                         start=(kp == 0),
@@ -444,106 +446,135 @@ def tile_attention_pb_t_kernel(
             nc.gpsimd.tensor_tensor(out=rstd[group][:], in0=mean_sq[:], in1=neg_half[:], op=ALU.pow)
 
         def finish(group):
-            b, half = divmod(group, TILES // GROUP)
             result = stage.tile([P, GROUP, HD], F32, name="result")
             for j in range(GROUP):
                 nc.vector.scalar_tensor_tensor(
-                    out=result[:, where(group * GROUP + j)[1] % GROUP, :],
+                    out=result[:, j, :],
                     in0=att[group][:, j, :],
                     scalar=rstd[group][:, j : j + 1],
                     in1=gain[:],
                     op0=ALU.mult,
                     op1=ALU.mult,
                 )
-            first = min(where(group * GROUP + j)[1] for j in range(GROUP)) * P
-            nc.sync.dma_start(
-                out=out[b, first : first + GROUP * P, 0, :].rearrange("(j p) d -> p j d", p=P), in_=result[:]
-            )
+            for j in range(GROUP):
+                b, it = where(group * GROUP + j)
+                nc.sync.dma_start(out=out[b, it * P : (it + 1) * P, 0, :], in_=result[:, j, :])
 
-        v_bank, v_grouped = {}, {}
+        STEPS = ITEMS // 2
+        PIECES = 4 * B
+
+        def lead(n):
+            for c in (1, 0):
+                pass
+
+        def look(s, kind, c):
+            n = 2 * s + kind
+            if 0 <= s < STEPS:
+                if is_direct(n):
+                    rounded_energies(n, c)
+                else:
+                    energies(n, c)
 
         def h_step(m):
-            return max(m // 2, m - H_AHEAD)
+            return max(m // 3, m // 2 - H_LEAD)
 
-        def at(s, offset, period):
-            k, r = divmod(s - offset, period)
-            return k if r == 0 and k >= 0 else None
+        def stages(s):
+            a, w = 2 * s, 2 * s + 1
+            live = 0 <= s < STEPS
+            direct = live and is_direct(w)
+            st = {}
 
-        for s in range(-TILES, ITEMS + 12):
-            b, it = divmod(s, TILES)
-            if it == 0:
+            def add(name, ok, *calls):
+                st[name] = calls if ok else ()
+
+            add("Ma", live, (scale_and_max, a, (1, 0)))
+            if direct:
+                add("Mw1", live, (row_max, w, 1))
+                add("Mw0", live, (row_max, w, 0))
+            else:
+                add("Mw1", live, (scale_and_max, w, (1, 0)))
+                add("Mw0", False)
+            add("Ew1", direct, (energies, w, 1))
+            add("Ew0a", direct, (energies, w, 0, slice(0, 1)))
+            add("Ew0b", direct, (energies, w, 0, slice(1, 2)))
+            add("Xa1", live, (exponentials, a, 1))
+            add("Xa0", live, (exponentials, a, 0))
+            add("Xw1", live, (exponentials, w, 1))
+            add("Xw0", live, (exponentials, w, 0))
+            add("PS", direct, (add_part_sums, s))
+            add("La1", True, (look, s + 1, 0, 1))
+            add("La0", True, (look, s + 1, 0, 0))
+            ahead = s + 1 < STEPS and is_direct(w + 2)
+            add("Lw1", ahead, (look, s + 1, 1, 1))
+            add("Lw0", ahead, (look, s + 1, 1, 0))
+            add("Ly", not ahead, (look, s + 1, 1, 1), (look, s + 1, 1, 0))
+            hm = [m for m in range(B * TILES) if h_step(m) == s]
+            for i in range(2):
+                mine = [m for m in hm if m % 2 == i]
+                add("H%dt" % i, live and mine, *[(transpose_h, m) for m in mine])
+                add("H%dc" % i, live and mine, *[(copy_h, m) for m in mine])
+            qh = [p for p in range(ITEMS // 2) if h_step(2 * p) + 1 == s]
+            add("QH", qh, *[(quantise_h, p) for p in qh])
+            pieces = [p for p in range(4, PIECES) if max(0, p - 5) == s]
+            add("QKt", True, *[(transpose_qk, p) for p in pieces])
+            add("QKc", True, *[(copy_qk, p, nc.scalar.copy) for p in pieces])
+            vg = [g for g in range(2 * B) if h_step(4 * g + 2) + V_AFTER == s]
+            add("Vt", vg, *[(project_v, g) for g in vg])
+            add("Vc", vg, *[(copy_v, g) for g in vg])
+            vq = [g for g in range(2 * B) if h_step(4 * g + 2) + V_AFTER + QV_AFTER == s]
+            add("QV", vq, *[(quantise_v, g) for g in vq])
+            r = s - R_LAG
+            ok = 0 <= r < STEPS
+            add("R", ok, (invert_sums, r))
+            wide_on_v = ok and where(2 * r + 1)[1] in W_ON_VECTOR
+            add("W", ok, (weigh_second, 2 * r, nc.gpsimd if r < STEPS - 2 else nc.vector), *([] if wide_on_v else [(weigh_second, 2 * r + 1, nc.gpsimd if r < STEPS - 2 else nc.vector)]))
+            k = s - CB_LAG
+            ok = 0 <= k < STEPS
+            add("WV", ok and where(2 * k + 1)[1] in W_ON_VECTOR, (weigh_second, 2 * k + 1, nc.vector))
+            add("CBa", ok, (combine, 2 * k))
+            add("CBw", ok, (combine, 2 * k + 1))
+            t = s - T_LAG
+            ok = 0 <= t < STEPS
+            add("Tw", ok, (transpose_sc, [2 * t + 1], 2 * t + 1))
+            add("Ta", ok and t % 2 == 1, (transpose_sc, [2 * t - 2, 2 * t], 2 * t))
+            t = s - CS_LAG
+            ok = 0 <= t < STEPS
+            add("CSw", ok, (copy_sc, 2 * t + 1, t // 2, 2 * (t % 2), nc.scalar.copy if where(2 * t + 1)[1] in SC_ON_SCALAR else nc.vector.tensor_copy) if ok else ())
+            add("CSa", ok and t % 2 == 1, (copy_sc, 2 * t, t // 2, 0, nc.vector.tensor_copy))
+            t = s - QS_LAG
+            ok = 0 <= t < STEPS and t % 2 == 1
+            add("QSw", ok, (quantise_sc, t // 2, 1))
+            add("QSa", ok, (quantise_sc, t // 2, 0))
+            t = s - ATT_LAG
+            ok = 0 <= t < STEPS and t % 2 == 1
+            add("At", ok, (attend, t // 2))
+            add("Sq", ok, (square_sums, t // 2))
+            add("RR", ok, (row_rms, t // 2))
+            t = s - F_LAG
+            ok = 0 <= t < STEPS and t % 2 == 1
+            add("F", ok, (finish, t // 2))
+            return st
+
+        for piece in range(4):
+            transpose_qk(piece)
+            copy_qk(piece, nc.vector.tensor_copy if piece % 2 else nc.scalar.copy)
+        for kind in (0, 1):
+            for c in (1, 0):
+                look(0, kind, c)
+        load_h(0)
+        load_qk(1)
+        for s in range(STEPS + 8):
+            b, j = divmod(s, 4)
+            if j == 0 and b + 1 < B:
                 if b + 2 < B:
                     load_qk(b + 2)
-                if b + 1 < B:
-                    load_h(b + 1)
-
-            live = is_item(s)
-            direct = live and is_direct(s)
-            if live:
-                if direct:
-                    row_max(s, 1)
-                    energies(s, 1)
-                else:
-                    scale_and_max(s, 1)
-                exponentials(s, 1)
-            if is_item(s - 3) and where(s - 3)[1] in SC_ON_SCALAR:
-                copy_sc(s - 3)
-            for m in range(B * TILES):
-                if h_step(m) == s:
-                    transpose_h(m)
-            qk_batch, qk_piece = divmod(s + TILES - QK_FROM, TILES)
-            if qk_piece < 4 and 0 <= qk_batch < B:
-                transpose_qk(qk_batch, qk_piece, nc.scalar.copy)
-            if s == 1:
-                words_to_k_major(wv_raw[:], wv_grouped[:])
-            if s == 3:
+                load_h(b + 1)
+            if s == WV_AT:
+                wv_bank = transpose_words(wv_raw[:])
+                copy_words(wv_bank, wv_grouped[:])
+            if s == WV_AT + 1:
                 quantise_wv()
-            if is_item(s - 3) and where(s - 3)[1] not in SC_ON_SCALAR:
-                copy_sc(s - 3)
-            f = at(s, FIN_AT, GROUP)
-            if f is not None and f < ITEMS // GROUP:
-                finish(f)
-            if is_item(s + 1):
-                if is_direct(s + 1):
-                    rounded_energies(s + 1, 1)
-                else:
-                    energies(s + 1, 1)
-            v_now = [vg for vg in range(2 * B) if h_step(4 * vg + 3) + V_AFTER == s]
-            for vg in v_now:
-                v_bank[vg] = project_v(vg)
-            group = at(s, ATT_AT, GROUP)
-            if group is not None and group < ITEMS // GROUP:
-                attend(group)
-            if live:
-                if direct:
-                    row_max(s, 0)
-                    energies(s, 0)
-                else:
-                    scale_and_max(s, 0)
-                exponentials(s, 0)
-            if is_item(s - 2):
-                combine(s - 2)
-                transpose_sc(s - 2)
-            if is_item(s + 1):
-                if is_direct(s + 1):
-                    rounded_energies(s + 1, 0)
-                else:
-                    energies(s + 1, 0)
-            for vg in v_now:
-                v_grouped[vg] = copy_v(v_bank[vg])
-            if group is not None and group < ITEMS // GROUP:
-                square_sums(group)
-            for pair in range(ITEMS // PAIR):
-                if h_step(PAIR * pair + 1) + 1 == s:
-                    quantise_h(pair)
-            for vg in range(2 * B):
-                if h_step(4 * vg + 3) + V_AFTER + 1 == s:
-                    quantise_v(vg, v_grouped[vg])
-            if s % PAIR == 0 and is_item(s - 3):
-                quantise_sc((s - 3) // PAIR)
-            if is_item(s - 1):
-                weigh_second(s - 1)
-            if direct:
-                add_part_sums(s)
-            if group is not None and group < ITEMS // GROUP:
-                row_rms(group)
+            st = stages(s)
+            for name in (ORDER if s < STEPS - 1 else TAIL_ORDER).split():
+                for call in st[name]:
+                    call[0](*call[1:])

@@ -22,7 +22,7 @@ K_PASS = 512
 ITEMS = B * TILES
 GROUP = 4
 PAIR = 2
-SC_ON_SCALAR = ()
+SC_ON_SCALAR = (4, 5, 6, 7)
 W_ON_VECTOR = ()
 EXPO_BUFS = 3
 H_LEAD, V_AFTER, QV_AFTER, WV_AT = 1, 2, 1, 0

@@ -22,13 +22,14 @@ K_PASS = 512
 ITEMS = B * TILES
 GROUP = 4
 PAIR = 2
-SC_ON_SCALAR = (4, 5, 6, 7)
+SC_ON_SCALAR = (6, 7)
 W_ON_VECTOR = ()
 EXPO_BUFS = 3
+QK_AT = (0, 1, 2, 2)
 H_LEAD, V_AFTER, QV_AFTER, WV_AT = 1, 2, 1, 0
 R_LAG, CB_LAG, T_LAG, CS_LAG, QS_LAG, ATT_LAG, F_LAG = 1, 2, 2, 3, 3, 5, 6
 TAIL_ORDER = """Ma Mw1 Mw0 Ew1 Ew0a Xa1 Xa0 Xw1 Ew0b Xw0 PS R W CSw CSa F Vt At Vc Sq RR CBw CBa Tw Ta QV QH QSw QSa"""
-ORDER = """Ma Mw1 Mw0 Ew1 Ew0a Xa1 Xa0 Xw1 Lw1 Ew0b Lw0 CSw CSa F Xw0 H0t H1t La1 QKt La0 H0c H1c QKc Vt At Vc Sq CBw CBa Tw Ta Ly QH QV QSw QSa R W PS RR WV"""
+ORDER = """Ma Mw1 Mw0 Ew1 Ew0a Xa1 Xa0 CSw Xw1 Lw1 Ew0b Lw0 CSa F Xw0 H0t H1t La1 QKt La0 H0c H1c QKc Vt At Ly Vc Sq CBw CBa Tw Ta QH QV QSw QSa R W PS RR WV"""
 DIRECT_FROM = 5
 SM_SCALE = 1.0 / math.sqrt(HD)
 LOG2_E = 1.0 / math.log(2.0)
@@ -515,7 +516,7 @@ def tile_attention_pb_t_kernel(
                 add("H%dc" % i, live and mine, *[(copy_h, m) for m in mine])
             qh = [p for p in range(ITEMS // 2) if h_step(2 * p) + 1 == s]
             add("QH", qh, *[(quantise_h, p) for p in qh])
-            pieces = [p for p in range(4, PIECES) if max(0, p - 5) == s]
+            pieces = [p for p in range(4, PIECES) if 4 * (p // 4 - 1) + QK_AT[p % 4] == s]
             add("QKt", True, *[(transpose_qk, p) for p in pieces])
             add("QKc", True, *[(copy_qk, p, nc.scalar.copy) for p in pieces])
             vg = [g for g in range(2 * B) if h_step(4 * g + 2) + V_AFTER == s]

@@ -22,14 +22,15 @@ K_PASS = 512
 ITEMS = B * TILES
 GROUP = 4
 PAIR = 2
-SC_ON_SCALAR = (6, 7)
-W_ON_VECTOR = ()
+SC_ON_SCALAR = (4, 7)
 EXPO_BUFS = 3
-QK_AT = (0, 1, 2, 2)
-H_LEAD, V_AFTER, QV_AFTER, WV_AT = 1, 2, 1, 0
-R_LAG, CB_LAG, T_LAG, CS_LAG, QS_LAG, ATT_LAG, F_LAG = 1, 2, 2, 3, 3, 5, 6
-TAIL_ORDER = """Ma Mw1 Mw0 Ew1 Ew0a Xa1 Xa0 Xw1 Ew0b Xw0 PS R W CSw CSa F Vt At Vc Sq RR CBw CBa Tw Ta QV QH QSw QSa"""
-ORDER = """Ma Mw1 Mw0 Ew1 Ew0a Xa1 Xa0 CSw Xw1 Lw1 Ew0b Lw0 CSa F Xw0 H0t H1t La1 QKt La0 H0c H1c QKc Vt At Ly Vc Sq CBw CBa Tw Ta QH QV QSw QSa R W PS RR WV"""
+CB_END, CS_END, ATT_END = 40, 40, 39
+HEAD = 0
+QK_AT = (0, 0, 1, 2)
+H_LEAD, V_AFTER, QV_AFTER, WV_AT = 0, 2, 1, 0
+R_LAG, CB_LAG, T_LAG, CS_LAG, QS_LAG, ATT_LAG, F_LAG = 1, 2, 2, 3, 3, 7, 8
+TAIL_ORDER = """Ma Mw1 Mw0 Ew1 Ew0a Xa1 Xa0 Xw1 Ew0b Xw0 PS R W CSw CSa F H0t H1t H0c H1c Vt At Vc Sq RR CBw CBa Tw Ta QV QH QSw QSa"""
+ORDER = """Ma Mw1 Mw0 Ew1 Ew0a Xa1 Xa0 CSw Xw1 Lw1 Ew0b Lw0 CSa F Xw0 H0t H1t La1 QKt La0 H0c H1c QKc Vt At Ly Vc Sq CBw CBa Tw Ta QH QV QSw QSa R W PS RR"""
 DIRECT_FROM = 5
 SM_SCALE = 1.0 / math.sqrt(HD)
 LOG2_E = 1.0 / math.log(2.0)
@@ -167,8 +168,8 @@ def tile_attention_pb_t_kernel(
                 nc.tensor.transpose(bank[:, w, :], words[:, w * P : (w + 1) * P], ident_f32[:])
             return bank
 
-        def copy_words(bank, grouped):
-            nc.scalar.copy(
+        def copy_words(bank, grouped, copy_out):
+            copy_out(
                 out=grouped.bitcast(F32), in_=bank[:].rearrange("p (g u) r -> p g r u", u=2)
             )
 
@@ -190,8 +191,8 @@ def tile_attention_pb_t_kernel(
                 h_grouped[m // PAIR] = stage.tile([P, PAIR, 2, P, 4], BF16, name="h_grouped", align_bytes=64)
             h_bank[m] = transpose_words(h_raw[b][:, g, t * D : (t + 1) * D])
 
-        def copy_h(m):
-            copy_words(h_bank[m], h_grouped[m // PAIR][:, m % PAIR])
+        def copy_h(m, copy_out):
+            copy_words(h_bank[m], h_grouped[m // PAIR][:, m % PAIR], copy_out)
 
         def quantise_h(pair):
             b, half = divmod(pair, TILES // PAIR)
@@ -484,6 +485,7 @@ def tile_attention_pb_t_kernel(
             live = 0 <= s < STEPS
             direct = live and is_direct(w)
             st = {}
+            spare = nc.vector.tensor_copy if s < HEAD else nc.scalar.copy
 
             def add(name, ok, *calls):
                 st[name] = calls if ok else ()
@@ -513,47 +515,44 @@ def tile_attention_pb_t_kernel(
             for i in range(2):
                 mine = [m for m in hm if m % 2 == i]
                 add("H%dt" % i, live and mine, *[(transpose_h, m) for m in mine])
-                add("H%dc" % i, live and mine, *[(copy_h, m) for m in mine])
-            qh = [p for p in range(ITEMS // 2) if h_step(2 * p) + 1 == s]
+                add("H%dc" % i, live and mine, *[(copy_h, m, spare) for m in mine])
+            qh = [p for p in range(ITEMS // 2) if h_step(2 * p + 1) + 1 == s]
             add("QH", qh, *[(quantise_h, p) for p in qh])
             pieces = [p for p in range(4, PIECES) if 4 * (p // 4 - 1) + QK_AT[p % 4] == s]
             add("QKt", True, *[(transpose_qk, p) for p in pieces])
-            add("QKc", True, *[(copy_qk, p, nc.scalar.copy) for p in pieces])
+            add("QKc", True, *[(copy_qk, p, spare) for p in pieces])
             vg = [g for g in range(2 * B) if h_step(4 * g + 2) + V_AFTER == s]
             add("Vt", vg, *[(project_v, g) for g in vg])
             add("Vc", vg, *[(copy_v, g) for g in vg])
             vq = [g for g in range(2 * B) if h_step(4 * g + 2) + V_AFTER + QV_AFTER == s]
             add("QV", vq, *[(quantise_v, g) for g in vq])
-            r = s - R_LAG
-            ok = 0 <= r < STEPS
-            add("R", ok, (invert_sums, r))
-            wide_on_v = ok and where(2 * r + 1)[1] in W_ON_VECTOR
-            add("W", ok, (weigh_second, 2 * r, nc.gpsimd if r < STEPS - 2 else nc.vector), *([] if wide_on_v else [(weigh_second, 2 * r + 1, nc.gpsimd if r < STEPS - 2 else nc.vector)]))
-            k = s - CB_LAG
-            ok = 0 <= k < STEPS
-            add("WV", ok and where(2 * k + 1)[1] in W_ON_VECTOR, (weigh_second, 2 * k + 1, nc.vector))
-            add("CBa", ok, (combine, 2 * k))
-            add("CBw", ok, (combine, 2 * k + 1))
-            t = s - T_LAG
-            ok = 0 <= t < STEPS
-            add("Tw", ok, (transpose_sc, [2 * t + 1], 2 * t + 1))
-            add("Ta", ok and t % 2 == 1, (transpose_sc, [2 * t - 2, 2 * t], 2 * t))
-            t = s - CS_LAG
-            ok = 0 <= t < STEPS
-            add("CSw", ok, (copy_sc, 2 * t + 1, t // 2, 2 * (t % 2), nc.scalar.copy if where(2 * t + 1)[1] in SC_ON_SCALAR else nc.vector.tensor_copy) if ok else ())
-            add("CSa", ok and t % 2 == 1, (copy_sc, 2 * t, t // 2, 0, nc.vector.tensor_copy))
-            t = s - QS_LAG
-            ok = 0 <= t < STEPS and t % 2 == 1
-            add("QSw", ok, (quantise_sc, t // 2, 1))
-            add("QSa", ok, (quantise_sc, t // 2, 0))
-            t = s - ATT_LAG
-            ok = 0 <= t < STEPS and t % 2 == 1
-            add("At", ok, (attend, t // 2))
-            add("Sq", ok, (square_sums, t // 2))
-            add("RR", ok, (row_rms, t // 2))
-            t = s - F_LAG
-            ok = 0 <= t < STEPS and t % 2 == 1
-            add("F", ok, (finish, t // 2))
+            def due(lag, limit=STEPS + 8):
+                return [t for t in range(STEPS) if min(t + lag, limit) == s]
+
+            def due_pairs(lag, limit=STEPS + 8):
+                return [t for t in due(lag, limit) if t % 2 == 1]
+
+            ts = due(R_LAG)
+            add("R", ts, *[(invert_sums, t) for t in ts])
+            add("W", ts, *[(weigh_second, n, nc.gpsimd if t < STEPS - 2 else nc.vector) for t in ts for n in (2 * t, 2 * t + 1)])
+            ts = due(CB_LAG, CB_END)
+            add("CBa", ts, *[(combine, 2 * t) for t in ts])
+            add("CBw", ts, *[(combine, 2 * t + 1) for t in ts])
+            add("Tw", ts, *[(transpose_sc, [2 * t + 1], 2 * t + 1) for t in ts])
+            add("Ta", ts, *[(transpose_sc, [2 * t - 2, 2 * t], 2 * t) for t in ts if t % 2 == 1])
+            ts = due(CS_LAG, CS_END)
+            late = nc.scalar.copy if s >= STEPS - 1 else nc.vector.tensor_copy
+            add("CSw", ts, *[(copy_sc, 2 * t + 1, t // 2, 2 * (t % 2), nc.scalar.copy if where(2 * t + 1)[1] in SC_ON_SCALAR else late) for t in ts])
+            add("CSa", ts, *[(copy_sc, 2 * t, t // 2, 0, late) for t in ts if t % 2 == 1])
+            ts = due_pairs(QS_LAG, CS_END)
+            add("QSw", ts, *[(quantise_sc, t // 2, 1) for t in ts])
+            add("QSa", ts, *[(quantise_sc, t // 2, 0) for t in ts])
+            ts = due_pairs(ATT_LAG, ATT_END)
+            add("At", ts, *[(attend, t // 2) for t in ts])
+            add("Sq", ts, *[(square_sums, t // 2) for t in ts])
+            add("RR", ts, *[(row_rms, t // 2) for t in ts])
+            ts = due_pairs(F_LAG, ATT_END + 1)
+            add("F", ts, *[(finish, t // 2) for t in ts])
             return st
 
         for piece in range(4):
@@ -570,12 +569,11 @@ def tile_attention_pb_t_kernel(
                 if b + 2 < B:
                     load_qk(b + 2)
                 load_h(b + 1)
-            if s == WV_AT:
-                wv_bank = transpose_words(wv_raw[:])
-                copy_words(wv_bank, wv_grouped[:])
-            if s == WV_AT + 1:
-                quantise_wv()
             st = stages(s)
             for name in (ORDER if s < STEPS - 1 else TAIL_ORDER).split():
                 for call in st[name]:
                     call[0](*call[1:])
+            if s == 0:
+                copy_words(transpose_words(wv_raw[:]), wv_grouped[:], nc.scalar.copy)
+            if s == 1:
+                quantise_wv()

@@ -22,7 +22,7 @@ K_PASS = 512
 ITEMS = B * TILES
 GROUP = 4
 PAIR = 2
-SC_ON_SCALAR = (4, 7)
+SC_ON_SCALAR = (7,)
 EXPO_BUFS = 3
 CB_END, CS_END, ATT_END = 40, 40, 39
 HEAD = 0
@@ -30,7 +30,7 @@ QK_AT = (0, 0, 1, 2)
 H_LEAD, V_AFTER, QV_AFTER, WV_AT = 0, 2, 1, 0
 R_LAG, CB_LAG, T_LAG, CS_LAG, QS_LAG, ATT_LAG, F_LAG = 1, 2, 2, 3, 3, 7, 8
 TAIL_ORDER = """Ma Mw1 Mw0 Ew1 Ew0a Xa1 Xa0 Xw1 Ew0b Xw0 PS R W CSw CSa F H0t H1t H0c H1c Vt At Vc Sq RR CBw CBa Tw Ta QV QH QSw QSa"""
-ORDER = """Ma Mw1 Mw0 Ew1 Ew0a Xa1 Xa0 CSw Xw1 Lw1 Ew0b Lw0 CSa F Xw0 H0t H1t La1 QKt La0 H0c H1c QKc Vt At Ly Vc Sq CBw CBa Tw Ta QH QV QSw QSa R W PS RR"""
+ORDER = """Ma Mw1 Mw0 Ew1 Xa1 Xa0 CSw Xw1 Lw1 Ew0a Ew0b Lw0 CSa F Xw0 H0t H1t La1 QKt La0 H0c H1c QKc Vt At Ly Vc Sq CBw CBa Tw Ta QH QV QSw QSa R W PS RR"""
 DIRECT_FROM = 5
 SM_SCALE = 1.0 / math.sqrt(HD)
 LOG2_E = 1.0 / math.log(2.0)
@@ -79,13 +79,13 @@ def tile_attention_pb_t_kernel(
 
         def load_qk(b):
             q_raw[b] = raw.tile([P, TILES, C * HD], BF16, name="q_raw")
-            nc.sync.dma_start(
-                out=q_raw[b][:], in_=q_rot[b, :, 0, :].rearrange("(t p) d -> p t d", p=P)
-            )
             k_raw[b] = raw.tile([P, TILES, C * HD], BF16, name="k_raw")
-            nc.sync.dma_start(
-                out=k_raw[b][:], in_=k_rot[b, :, 0, :].rearrange("(t p) d -> p t d", p=P)
-            )
+            parts = 2 if b == 0 else 1
+            for i in range(parts):
+                tiles = slice(i * TILES // parts, (i + 1) * TILES // parts)
+                rows = slice(i * S // parts, (i + 1) * S // parts)
+                for dst, src in ((q_raw[b], q_rot), (k_raw[b], k_rot)):
+                    nc.sync.dma_start(out=dst[:, tiles, :], in_=src[b, rows, 0, :].rearrange("(t p) d -> p t d", p=P))
 
         rows = const.tile([P, 6 * P], BF16, name="rows")
         nc.vector.memset(rows[:], 0.0)
@@ -93,6 +93,9 @@ def tile_attention_pb_t_kernel(
             nc.scalar.dma_start(out=rows[0:1, i * P : (i + 1) * P], in_=vec.rearrange("h d o -> h (d o)"))
         nc.scalar.dma_start(out=rows[0:1, 4 * P : 5 * P], in_=head_norm_w.rearrange("(o d) -> o d", o=1))
         nc.scalar.dma_start(out=rows[0:1, 5 * P : 5 * P + 1], in_=lam_init.rearrange("(o d) -> o d", o=1))
+        warm = const.tile([P, 1], F32, name="warm")
+        nc.vector.memset(warm[:], 0.0)
+        nc.scalar.activation(out=warm[:], in_=warm[:], func=ACT.Exp)
         load_qk(0)
         wv_raw = const.tile([P, D], BF16, name="wv_raw")
         nc.sync.dma_start(out=wv_raw[:], in_=wv)
@@ -458,7 +461,6 @@ def tile_attention_pb_t_kernel(
                     op0=ALU.mult,
                     op1=ALU.mult,
                 )
-            for j in range(GROUP):
                 b, it = where(group * GROUP + j)
                 nc.sync.dma_start(out=out[b, it * P : (it + 1) * P, 0, :], in_=result[:, j, :])
 
@@ -543,7 +545,7 @@ def tile_attention_pb_t_kernel(
             ts = due(CS_LAG, CS_END)
             late = nc.scalar.copy if s >= STEPS - 1 else nc.vector.tensor_copy
             add("CSw", ts, *[(copy_sc, 2 * t + 1, t // 2, 2 * (t % 2), nc.scalar.copy if where(2 * t + 1)[1] in SC_ON_SCALAR else late) for t in ts])
-            add("CSa", ts, *[(copy_sc, 2 * t, t // 2, 0, late) for t in ts if t % 2 == 1])
+            add("CSa", ts, *[(copy_sc, 2 * t, t // 2, 0, nc.scalar.copy if t % 4 == 3 else late) for t in ts if t % 2 == 1])
             ts = due_pairs(QS_LAG, CS_END)
             add("QSw", ts, *[(quantise_sc, t // 2, 1) for t in ts])
             add("QSa", ts, *[(quantise_sc, t // 2, 0) for t in ts])

@@ -20,18 +20,11 @@ TILES = S // P
 BANK = 512
 K_PASS = 512
 ITEMS = B * TILES
+STEPS = ITEMS // 2
+BATCH_STEPS = TILES // 2
 GROUP = 4
 PAIR = 2
-SC_ON_SCALAR = (7,)
-EXPO_BUFS = 3
-CB_END, CS_END, ATT_END = 40, 40, 39
-HEAD = 0
-QK_AT = (0, 0, 1, 2)
-H_LEAD, V_AFTER, QV_AFTER, WV_AT = 0, 2, 1, 0
-R_LAG, CB_LAG, T_LAG, CS_LAG, QS_LAG, ATT_LAG, F_LAG = 1, 2, 2, 3, 3, 7, 8
-TAIL_ORDER = """Ma Mw1 Mw0 Ew1 Ew0a Xa1 Xa0 Xw1 Ew0b Xw0 PS R W CSw CSa F H0t H1t H0c H1c Vt At Vc Sq RR CBw CBa Tw Ta QV QH QSw QSa"""
-ORDER = """Ma Mw1 Mw0 Ew1 Xa1 Xa0 CSw Xw1 Lw1 Ew0a Ew0b Lw0 CSa F Xw0 H0t H1t La1 QKt La0 H0c H1c QKc Vt At Ly Vc Sq CBw CBa Tw Ta QH QV QSw QSa R W PS RR"""
-DIRECT_FROM = 5
+FROM_PSUM = 5
 SM_SCALE = 1.0 / math.sqrt(HD)
 LOG2_E = 1.0 / math.log(2.0)
 MASKED = -1.0e30
@@ -41,6 +34,43 @@ FLOPS = 2 * B * S * D * HD + 2 * B * C * S * S * HD + 2 * B * S * S * HD
 
 def key_passes(it):
     return (it * P) // K_PASS + 1
+
+
+def narrow(step):
+    return 2 * step
+
+
+def wide(step):
+    return 2 * step + 1
+
+
+def is_wide(n):
+    return n % 2 == 1
+
+
+def locate(n):
+    b, i = divmod(n, TILES)
+    return b, (TILES - 1 - i // 2 if is_wide(n) else i // 2)
+
+
+def row_width(n):
+    return (locate(n)[1] + 1) * P
+
+
+def key_runs(n):
+    return [(lo, min(BANK, row_width(n) - lo)) for lo in range(0, row_width(n), BANK)]
+
+
+def from_psum(n):
+    return locate(n)[1] >= FROM_PSUM
+
+
+def due(step, lag):
+    return [step - lag] if 0 <= step - lag < STEPS else []
+
+
+def group_due(step, lag):
+    return [t // 2 for t in due(step, lag) if t % 2 == 1]
 
 
 def tile_attention_pb_t_kernel(
@@ -54,20 +84,19 @@ def tile_attention_pb_t_kernel(
         batch = ctx.enter_context(tc.tile_pool(name="batch", bufs=2))
         stage = ctx.enter_context(tc.tile_pool(name="stage", bufs=3))
         soft = ctx.enter_context(tc.tile_pool(name="soft", bufs=2))
+        expos = ctx.enter_context(tc.tile_pool(name="expos", bufs=3))
         stat = ctx.enter_context(tc.tile_pool(name="stat", bufs=4))
-        codes = ctx.enter_context(tc.tile_pool(name="codes", bufs=6))
+        codes = ctx.enter_context(tc.tile_pool(name="codes", bufs=3))
         psum_e = ctx.enter_context(tc.psum_pool(name="psum_e", bufs=3))
         psum_r = ctx.enter_context(tc.psum_pool(name="psum_r", bufs=2))
         psum_in = ctx.enter_context(tc.psum_pool(name="psum_in", bufs=3))
-        psum_sc = psum_in
 
-        h_raw, q_raw, k_raw, h_bank, qk_bank, v_bank, v_grouped = {}, {}, {}, {}, {}, {}, {}
-        h_grouped, h_codes, h_scales = {}, {}, {}
-        q_t, k_t = {}, {}
-        v_codes, v_scales = {}, {}
-        energy, rounded, neg_max, y, expo, sums, inv = {}, {}, {}, {}, {}, {}, {}
+        q_raw, k_raw, q_t, k_t, qk_bank = {}, {}, {}, {}, {}
+        h_raw, h_bank, h_grouped, h_codes, h_scales = {}, {}, {}, {}, {}
+        v_bank, v_grouped, v_codes, v_scales = {}, {}, {}, {}
+        energy, rounded, neg_max, y, expo, part_sums, sums, inv = {}, {}, {}, {}, {}, {}, {}, {}
         sc_bank, sc_grouped, sc_codes, sc_scales = {}, {}, {}, {}
-        att, sum_sq, rstd, part_sums = {}, {}, {}, {}
+        att, sum_sq, rstd = {}, {}, {}
 
         def load_h(b):
             h_raw[b] = raw.tile([P, 2, 4 * D], BF16, name="h_raw")
@@ -83,9 +112,11 @@ def tile_attention_pb_t_kernel(
             parts = 2 if b == 0 else 1
             for i in range(parts):
                 tiles = slice(i * TILES // parts, (i + 1) * TILES // parts)
-                rows = slice(i * S // parts, (i + 1) * S // parts)
+                tokens = slice(i * S // parts, (i + 1) * S // parts)
                 for dst, src in ((q_raw[b], q_rot), (k_raw[b], k_rot)):
-                    nc.sync.dma_start(out=dst[:, tiles, :], in_=src[b, rows, 0, :].rearrange("(t p) d -> p t d", p=P))
+                    nc.sync.dma_start(
+                        out=dst[:, tiles, :], in_=src[b, tokens, 0, :].rearrange("(t p) d -> p t d", p=P)
+                    )
 
         rows = const.tile([P, 6 * P], BF16, name="rows")
         nc.vector.memset(rows[:], 0.0)
@@ -93,9 +124,9 @@ def tile_attention_pb_t_kernel(
             nc.scalar.dma_start(out=rows[0:1, i * P : (i + 1) * P], in_=vec.rearrange("h d o -> h (d o)"))
         nc.scalar.dma_start(out=rows[0:1, 4 * P : 5 * P], in_=head_norm_w.rearrange("(o d) -> o d", o=1))
         nc.scalar.dma_start(out=rows[0:1, 5 * P : 5 * P + 1], in_=lam_init.rearrange("(o d) -> o d", o=1))
-        warm = const.tile([P, 1], F32, name="warm")
-        nc.vector.memset(warm[:], 0.0)
-        nc.scalar.activation(out=warm[:], in_=warm[:], func=ACT.Exp)
+        first_exp = const.tile([P, 1], F32, name="first_exp")
+        nc.vector.memset(first_exp[:], 0.0)
+        nc.scalar.activation(out=first_exp[:], in_=first_exp[:], func=ACT.Exp)
         load_qk(0)
         wv_raw = const.tile([P, D], BF16, name="wv_raw")
         nc.sync.dma_start(out=wv_raw[:], in_=wv)
@@ -171,10 +202,8 @@ def tile_attention_pb_t_kernel(
                 nc.tensor.transpose(bank[:, w, :], words[:, w * P : (w + 1) * P], ident_f32[:])
             return bank
 
-        def copy_words(bank, grouped, copy_out):
-            copy_out(
-                out=grouped.bitcast(F32), in_=bank[:].rearrange("p (g u) r -> p g r u", u=2)
-            )
+        def copy_words(bank, grouped):
+            nc.scalar.copy(out=grouped.bitcast(F32), in_=bank[:].rearrange("p (g u) r -> p g r u", u=2))
 
         wv_grouped = const.tile([P, 2, P, 4], BF16, name="wv_grouped", align_bytes=64)
         wv_codes = const.tile([P, 2, P], U32, name="wv_codes", align_bytes=64)
@@ -187,90 +216,94 @@ def tile_attention_pb_t_kernel(
                 in_=wv_grouped[:].rearrange("p g r t -> p (g r t)"),
             )
 
-        def transpose_h(m):
-            b, st = divmod(m, TILES)
-            g, t = divmod(st, 4)
-            if m % PAIR == 0:
-                h_grouped[m // PAIR] = stage.tile([P, PAIR, 2, P, 4], BF16, name="h_grouped", align_bytes=64)
-            h_bank[m] = transpose_words(h_raw[b][:, g, t * D : (t + 1) * D])
+        def transpose_h(s, i):
+            for t in due(s, 0):
+                b, st = divmod(PAIR * t + i, TILES)
+                g, slot = divmod(st, 4)
+                if i == 0:
+                    h_grouped[t] = stage.tile([P, PAIR, 2, P, 4], BF16, name="h_grouped", align_bytes=64)
+                h_bank[t, i] = transpose_words(h_raw[b][:, g, slot * D : (slot + 1) * D])
 
-        def copy_h(m, copy_out):
-            copy_words(h_bank[m], h_grouped[m // PAIR][:, m % PAIR], copy_out)
+        def copy_h(s, i):
+            for t in due(s, 0):
+                copy_words(h_bank[t, i], h_grouped[t][:, i])
 
-        def quantise_h(pair):
-            b, half = divmod(pair, TILES // PAIR)
-            st = half * PAIR
-            if half == 0:
-                h_codes[b] = batch.tile([P, TILES, 2, P], U32, name="h_codes", align_bytes=64)
-                h_scales[b] = batch.tile([P, TILES, 2, P], U8, name="h_scales", align_bytes=64)
-            nc.vector.quantize_mx(
-                out=h_codes[b][:, st : st + PAIR].rearrange("p i g r -> p (i g r)").bitcast(FP8X4),
-                scales=h_scales[b][:, st : st + PAIR].rearrange("p i g r -> p (i g r)"),
-                in_=h_grouped[pair][:].rearrange("p i g r t -> p (i g r t)"),
-            )
+        def quantise_h(s):
+            for t in due(s, 1):
+                b, st = divmod(PAIR * t, TILES)
+                if st == 0:
+                    h_codes[b] = batch.tile([P, TILES, 2, P], U32, name="h_codes", align_bytes=64)
+                    h_scales[b] = batch.tile([P, TILES, 2, P], U8, name="h_scales", align_bytes=64)
+                nc.vector.quantize_mx(
+                    out=h_codes[b][:, st : st + PAIR].rearrange("p i g r -> p (i g r)").bitcast(FP8X4),
+                    scales=h_scales[b][:, st : st + PAIR].rearrange("p i g r -> p (i g r)"),
+                    in_=h_grouped[t][:].rearrange("p i g r t -> p (i g r t)"),
+                )
 
-        def project_v(vg):
-            b, kp = divmod(vg, 2)
-            v_bank[vg] = psum_in.tile([P, 4, HD], F32, name="v_bank", tag="tin")
-            for t in range(4):
-                st = 4 * kp + t
-                for g in range(2):
-                    nc.tensor.matmul_mx(
-                        out=v_bank[vg][:, t, :],
-                        lhsT=h_codes[b][:, st, g, :].bitcast(FP8X4),
-                        lhsT_scale=h_scales[b][:, st, g, :],
-                        rhs=wv_codes[:, g, :].bitcast(FP8X4),
-                        rhs_scale=wv_scales[:, g, :],
-                        start=(g == 0),
-                        stop=(g == 1),
-                    )
+        def project_v(s):
+            for vg in group_due(s, 2):
+                b, kp = divmod(vg, 2)
+                v_bank[vg] = psum_in.tile([P, 4, HD], F32, name="v_bank", tag="tin")
+                for t in range(4):
+                    st = 4 * kp + t
+                    for g in range(2):
+                        nc.tensor.matmul_mx(
+                            out=v_bank[vg][:, t, :],
+                            lhsT=h_codes[b][:, st, g, :].bitcast(FP8X4),
+                            lhsT_scale=h_scales[b][:, st, g, :],
+                            rhs=wv_codes[:, g, :].bitcast(FP8X4),
+                            rhs_scale=wv_scales[:, g, :],
+                            start=(g == 0),
+                            stop=(g == 1),
+                        )
 
-        def copy_v(vg):
-            v_grouped[vg] = stage.tile([P, HD, 4], BF16, name="v_grouped", align_bytes=64)
-            nc.scalar.copy(out=v_grouped[vg][:], in_=v_bank[vg][:].rearrange("p t d -> p d t"))
+        def copy_v(s):
+            for vg in group_due(s, 2):
+                v_grouped[vg] = stage.tile([P, HD, 4], BF16, name="v_grouped", align_bytes=64)
+                nc.scalar.copy(out=v_grouped[vg][:], in_=v_bank[vg][:].rearrange("p t d -> p d t"))
 
-        def quantise_v(vg):
-            b, kp = divmod(vg, 2)
-            if kp == 0:
-                v_codes[b] = batch.tile([P, 2, HD], U32, name="v_codes", align_bytes=64)
-                v_scales[b] = batch.tile([P, 2, HD], U8, name="v_scales", align_bytes=64)
-            nc.vector.quantize_mx(
-                out=v_codes[b][:, kp, :].bitcast(FP8X4),
-                scales=v_scales[b][:, kp, :],
-                in_=v_grouped[vg][:].rearrange("p d t -> p (d t)"),
-            )
+        def quantise_v(s):
+            for vg in group_due(s, 3):
+                b, kp = divmod(vg, 2)
+                if kp == 0:
+                    v_codes[b] = batch.tile([P, 2, HD], U32, name="v_codes", align_bytes=64)
+                    v_scales[b] = batch.tile([P, 2, HD], U8, name="v_scales", align_bytes=64)
+                nc.vector.quantize_mx(
+                    out=v_codes[b][:, kp, :].bitcast(FP8X4),
+                    scales=v_scales[b][:, kp, :],
+                    in_=v_grouped[vg][:].rearrange("p d t -> p (d t)"),
+                )
 
-        def transpose_qk(piece):
-            b, i = divmod(piece, 4)
+        def transpose_piece(b, i):
             c, is_k = 1 - i // 2, i % 2
             if i == 0:
                 q_t[b] = batch.tile([P, C, S], BF16, name="q_t")
                 k_t[b] = batch.tile([P, C, S], BF16, name="k_t")
             src = k_raw[b] if is_k else q_raw[b]
-            qk_bank[piece] = psum_in.tile([P, TILES, P], BF16, name="qk_bank", tag="tin")
+            qk_bank[b, i] = psum_in.tile([P, TILES, P], BF16, name="qk_bank", tag="tin")
             for t in range(TILES):
-                nc.tensor.transpose(qk_bank[piece][:, t, :], src[:, t, c * HD : (c + 1) * HD], ident_bf[:])
+                nc.tensor.transpose(qk_bank[b, i][:, t, :], src[:, t, c * HD : (c + 1) * HD], ident_bf[:])
 
-        def copy_qk(piece, copy_out):
-            b, i = divmod(piece, 4)
+        def copy_piece(b, i, copy_out):
             c, is_k = 1 - i // 2, i % 2
             dst = k_t[b] if is_k else q_t[b]
-            copy_out(out=dst[:, c, :], in_=qk_bank[piece][:].rearrange("p t r -> p (t r)"))
+            copy_out(out=dst[:, c, :], in_=qk_bank[b, i][:].rearrange("p t r -> p (t r)"))
 
-        def where(n):
-            b, i = divmod(n, TILES)
-            return b, (i // 2 if i % 2 == 0 else TILES - 1 - i // 2)
+        def pieces_due(s):
+            b, j = divmod(s, BATCH_STEPS)
+            return [(b + 1, i) for i in range(4) if max(0, i - 1) == j and b + 1 < B]
 
-        def is_direct(n):
-            return where(n)[1] >= DIRECT_FROM
+        def transpose_qk(s):
+            for b, i in pieces_due(s):
+                transpose_piece(b, i)
 
-        def key_runs(n):
-            width = (where(n)[1] + 1) * P
-            return [(lo, min(BANK, width - lo)) for lo in range(0, width, BANK)]
+        def copy_qk(s):
+            for b, i in pieces_due(s):
+                copy_piece(b, i, nc.scalar.copy)
 
         def multiply_qk(n, c, lo, cols, dst):
-            b, it = where(n)
-            has_diagonal = lo + cols == (it + 1) * P
+            b, it = locate(n)
+            has_diagonal = lo + cols == row_width(n)
             nc.tensor.matmul(
                 dst,
                 lhsT=q_t[b][:, c, it * P : (it + 1) * P],
@@ -281,36 +314,42 @@ def tile_attention_pb_t_kernel(
             if has_diagonal:
                 nc.tensor.matmul(dst[:, cols - P :], lhsT=ident_bf[:], rhs=mask_bf[:], start=False, stop=True)
 
+        def energies(n, c):
+            for lo, cols in key_runs(n):
+                bank = psum_e.tile([P, BANK], F32, name="energy")
+                energy[n, c, lo] = bank[:, :cols]
+                multiply_qk(n, c, lo, cols, energy[n, c, lo])
+
         def rounded_energies(n, c):
             rounded[n, c] = psum_r.tile([P, S], BF16, name="rounded")
             for lo, cols in key_runs(n):
                 multiply_qk(n, c, lo, cols, rounded[n, c][:, lo : lo + cols])
 
-        def energies(n, c, runs=slice(None)):
-            for lo, cols in key_runs(n)[runs]:
-                bank = psum_e.tile([P, BANK], F32, name="energy")
-                energy[n, c, lo] = bank[:, :cols]
-                multiply_qk(n, c, lo, cols, energy[n, c, lo])
+        def energies_of_wide(s, c):
+            for t in due(s, 0):
+                if from_psum(wide(t)):
+                    energies(wide(t), c)
 
-        def row_max(n, c):
-            width = (where(n)[1] + 1) * P
-            neg_max[n, c] = stat.tile([P, 1], F32, name="neg_max%d" % c)
-            unused = soft.tile([P, S], BF16, name="unused")
-            nc.vector.tensor_scalar(
-                out=unused[:, :width],
-                in0=rounded[n, c][:, :width],
-                scalar1=-SM_SCALE,
-                scalar2=None,
-                op0=ALU.mult,
-                op1=ALU.min,
-                accum_out=neg_max[n, c][:],
-            )
+        def next_narrow(s, c):
+            for t in due(s + 1, 0):
+                energies(narrow(t), c)
 
-        def scale_and_max(n, components):
-            for c in components:
-                y[n, c] = soft.tile([P, DIRECT_FROM * P], F32, name="y%d" % c)
+        def next_rounded(s, c):
+            for t in due(s + 1, 0):
+                if from_psum(wide(t)):
+                    rounded_energies(wide(t), c)
+
+        def next_wide(s):
+            for t in due(s + 1, 0):
+                if not from_psum(wide(t)):
+                    for c in (1, 0):
+                        energies(wide(t), c)
+
+        def scale_and_max(n):
+            for c in (1, 0):
+                y[n, c] = soft.tile([P, FROM_PSUM * P], F32, name="y%d" % c)
             for lo, cols in key_runs(n):
-                for c in components:
+                for c in (1, 0):
                     so_far = neg_max[n, c][:] if lo > 0 else None
                     neg_max[n, c] = stat.tile([P, 1], F32, name="neg_max%d" % c)
                     nc.vector.tensor_scalar(
@@ -323,15 +362,42 @@ def tile_attention_pb_t_kernel(
                         accum_out=neg_max[n, c][:],
                     )
 
+        def row_max(n, c):
+            neg_max[n, c] = stat.tile([P, 1], F32, name="neg_max%d" % c)
+            unused = soft.tile([P, S], BF16, name="unused")
+            nc.vector.tensor_scalar(
+                out=unused[:, : row_width(n)],
+                in0=rounded[n, c][:, : row_width(n)],
+                scalar1=-SM_SCALE,
+                scalar2=None,
+                op0=ALU.mult,
+                op1=ALU.min,
+                accum_out=neg_max[n, c][:],
+            )
+
+        def max_narrow(s):
+            for t in due(s, 0):
+                scale_and_max(narrow(t))
+
+        def max_wide(s):
+            for t in due(s, 0):
+                if from_psum(wide(t)):
+                    for c in (1, 0):
+                        row_max(wide(t), c)
+                else:
+                    scale_and_max(wide(t))
+
         def exponentials(n, c):
-            step, wide = divmod(n, 2)
-            width = (where(n)[1] + 1) * P
-            expo[n, c] = soft.tile([P, S if wide else BANK], F32, name="expo%d%d" % (wide, c), bufs=EXPO_BUFS)
-            if step not in sums:
-                sums[step] = stat.tile([P, 2, C], F32, name="sums")
-            if is_direct(n):
-                if step not in part_sums:
-                    part_sums[step] = stat.tile([P, 2, C], F32, name="part")
+            t = n // 2
+            width = row_width(n)
+            expo[n, c] = expos.tile(
+                [P, S if is_wide(n) else BANK], F32, name="expo%d%d" % (1 if is_wide(n) else 0, c)
+            )
+            if t not in sums:
+                sums[t] = stat.tile([P, 2, C], F32, name="sums")
+            if from_psum(n):
+                if t not in part_sums:
+                    part_sums[t] = stat.tile([P, 2, C], F32, name="part_sums")
                 for lo, cols in key_runs(n):
                     nc.scalar.activation(
                         out=expo[n, c][:, lo : lo + cols],
@@ -339,7 +405,7 @@ def tile_attention_pb_t_kernel(
                         func=ACT.Exp,
                         bias=neg_max[n, c][:],
                         scale=SM_SCALE,
-                        accum_out=part_sums[step][:, lo // BANK, c : c + 1],
+                        accum_out=part_sums[t][:, lo // BANK, c : c + 1],
                     )
             else:
                 nc.scalar.activation(
@@ -348,234 +414,246 @@ def tile_attention_pb_t_kernel(
                     func=ACT.Exp,
                     bias=neg_max[n, c][:],
                     scale=-1.0,
-                    accum_out=sums[step][:, wide, c : c + 1],
+                    accum_out=sums[t][:, n % 2, c : c + 1],
                 )
 
-        def add_part_sums(step):
-            part = part_sums[step]
-            nc.gpsimd.tensor_tensor(out=sums[step][:, 1, :], in0=part[:, 0, :], in1=part[:, 1, :], op=ALU.add)
+        def exp_narrow(s):
+            for t in due(s, 0):
+                for c in (1, 0):
+                    exponentials(narrow(t), c)
 
-        def invert_sums(step):
-            inv[step] = stat.tile([P, 2, C], F32, name="inv")
-            nc.vector.reciprocal(out=inv[step][:].rearrange("p i c -> p (i c)"), in_=sums[step][:].rearrange("p i c -> p (i c)"))
+        def exp_wide(s, c):
+            for t in due(s, 0):
+                exponentials(wide(t), c)
 
-        def weigh_second(n, engine):
-            step, wide = divmod(n, 2)
-            width = (where(n)[1] + 1) * P
-            engine.tensor_scalar(
-                out=expo[n, 1][:, :width],
-                in0=expo[n, 1][:, :width],
-                scalar1=inv[step][:, wide, 1:2],
-                scalar2=scale[:],
-                op0=ALU.mult,
-                op1=ALU.mult,
-            )
+        def add_part_sums(s):
+            for t in due(s, 0):
+                if from_psum(wide(t)):
+                    nc.gpsimd.tensor_tensor(
+                        out=sums[t][:, 1, :], in0=part_sums[t][:, 0, :], in1=part_sums[t][:, 1, :], op=ALU.add
+                    )
 
-        def combine(n):
-            step, wide = divmod(n, 2)
-            b, it = where(n)
-            width = (it + 1) * P
-            nc.vector.scalar_tensor_tensor(
-                out=sc_rows[it][:, :width],
-                in0=expo[n, 0][:, :width],
-                scalar=inv[step][:, wide, 0:1],
-                in1=expo[n, 1][:, :width],
-                op0=ALU.mult,
-                op1=ALU.add,
-            )
+        def invert_sums(s):
+            for t in due(s, 1):
+                inv[t] = stat.tile([P, 2, C], F32, name="inv")
+                nc.vector.reciprocal(
+                    out=inv[t][:].rearrange("p i c -> p (i c)"), in_=sums[t][:].rearrange("p i c -> p (i c)")
+                )
 
-        def transpose_sc(items, key):
-            sc_bank[key] = psum_sc.tile([P, 4, P], F32, name="sc_bank", tag="tin")
+        def weigh_second(s):
+            for t in due(s, 1):
+                engine = nc.gpsimd if t < STEPS - 2 else nc.vector
+                for n in (narrow(t), wide(t)):
+                    engine.tensor_scalar(
+                        out=expo[n, 1][:, : row_width(n)],
+                        in0=expo[n, 1][:, : row_width(n)],
+                        scalar1=inv[t][:, n % 2, 1:2],
+                        scalar2=scale[:],
+                        op0=ALU.mult,
+                        op1=ALU.mult,
+                    )
+
+        def combine(s):
+            for t in due(s, 2):
+                for n in (wide(t), narrow(t)):
+                    width = row_width(n)
+                    nc.vector.scalar_tensor_tensor(
+                        out=sc_rows[locate(n)[1]][:, :width],
+                        in0=expo[n, 0][:, :width],
+                        scalar=inv[t][:, n % 2, 0:1],
+                        in1=expo[n, 1][:, :width],
+                        op0=ALU.mult,
+                        op1=ALU.add,
+                    )
+
+        def transpose_sc_of(items, key):
+            sc_bank[key] = psum_in.tile([P, 4, P], F32, name="sc_bank", tag="tin")
             slot = 0
             for n in items:
-                words = sc_rows[where(n)[1]][:].bitcast(F32)
-                for g in range(key_passes(where(n)[1])):
+                words = sc_rows[locate(n)[1]][:].bitcast(F32)
+                for g in range(key_passes(locate(n)[1])):
                     for u in range(2):
                         nc.tensor.transpose(
                             sc_bank[key][:, slot, :], words[:, 2 * P * g + u : 2 * P * (g + 1) : 2], ident_f32[:]
                         )
                         slot += 1
 
-        def copy_sc(key, pair, first, copy_out):
-            wide = key % 2
+        def transpose_sc(s):
+            for t in due(s, 2):
+                transpose_sc_of([wide(t)], wide(t))
+                if t % 2 == 1:
+                    transpose_sc_of([narrow(t - 1), narrow(t)], narrow(t))
+
+        def copy_sc_of(key, first, blocks, copy_out):
+            group = key // GROUP
             if first == 0:
-                sc_grouped[pair, wide] = stage.tile([P, 4 if wide else 2, P, 4], BF16, name="sc_grouped%d" % wide, align_bytes=64)
+                sc_grouped[group, key % 2] = stage.tile(
+                    [P, blocks, P, 4], BF16, name="sc_grouped%d" % (key % 2), align_bytes=64
+                )
             copy_out(
-                out=sc_grouped[pair, wide][:, first : first + 2].bitcast(F32),
+                out=sc_grouped[group, key % 2][:, first : first + 2].bitcast(F32),
                 in_=sc_bank[key][:].rearrange("p (g u) r -> p g r u", u=2),
             )
 
-        def quantise_sc(pair, wide):
-            blocks = 4 if wide else 2
-            sc_codes[pair, wide] = codes.tile([P, blocks, P], U32, name="sc_codes%d" % wide, align_bytes=64)
-            sc_scales[pair, wide] = codes.tile([P, blocks, P], U8, name="sc_scales%d" % wide, align_bytes=64)
-            nc.vector.quantize_mx(
-                out=sc_codes[pair, wide][:].rearrange("p g r -> p (g r)").bitcast(FP8X4),
-                scales=sc_scales[pair, wide][:].rearrange("p g r -> p (g r)"),
-                in_=sc_grouped[pair, wide][:].rearrange("p g r t -> p (g r t)"),
-            )
+        def copy_sc_wide(s):
+            scalar_takes = s % BATCH_STEPS == 0 or s >= STEPS - 1
+            for t in due(s, 3):
+                copy_sc_of(wide(t), 2 * (t % 2), 4, nc.scalar.copy if scalar_takes else nc.vector.tensor_copy)
 
-        def attend(group):
-            b = group // 2
-            att[group] = psum_in.tile([P, GROUP, HD], F32, name="att", tag="tin")
-            for j in range(GROUP):
-                n = group * GROUP + j
-                wide = n % 2
-                passes = 2 if wide else 1
-                for kp in range(passes):
-                    block = (j // 2) * passes + kp
-                    nc.tensor.matmul_mx(
-                        out=att[group][:, j, :],
-                        lhsT=sc_codes[group, wide][:, block, :].bitcast(FP8X4),
-                        lhsT_scale=sc_scales[group, wide][:, block, :],
-                        rhs=v_codes[b][:, kp, :].bitcast(FP8X4),
-                        rhs_scale=v_scales[b][:, kp, :],
-                        start=(kp == 0),
-                        stop=(kp == passes - 1),
+        def copy_sc_narrow(s):
+            scalar_takes = s % BATCH_STEPS == 2 or s >= STEPS - 1
+            for t in due(s, 3):
+                if t % 2 == 1:
+                    copy_sc_of(narrow(t), 0, 2, nc.scalar.copy if scalar_takes else nc.vector.tensor_copy)
+
+        def quantise_sc(s):
+            for group in group_due(s, 3):
+                for kind, blocks in ((1, 4), (0, 2)):
+                    sc_codes[group, kind] = codes.tile([P, blocks, P], U32, name="sc_codes%d" % kind, align_bytes=64)
+                    sc_scales[group, kind] = codes.tile([P, blocks, P], U8, name="sc_scales%d" % kind, align_bytes=64)
+                    nc.vector.quantize_mx(
+                        out=sc_codes[group, kind][:].rearrange("p g r -> p (g r)").bitcast(FP8X4),
+                        scales=sc_scales[group, kind][:].rearrange("p g r -> p (g r)"),
+                        in_=sc_grouped[group, kind][:].rearrange("p g r t -> p (g r t)"),
                     )
 
-        def square_sums(group):
-            squares = stage.tile([P, GROUP, HD], F32, name="squares")
-            sum_sq[group] = stat.tile([P, GROUP], F32, name="sum_sq")
-            for j in range(GROUP):
-                nc.scalar.activation(
-                    out=squares[:, j, :], in_=att[group][:, j, :], func=ACT.Square, accum_out=sum_sq[group][:, j : j + 1]
+        def attend(s):
+            for group in group_due(s, 7):
+                att[group] = psum_in.tile([P, GROUP, HD], F32, name="att", tag="tin")
+                for j in range(GROUP):
+                    n = group * GROUP + j
+                    b, it = locate(n)
+                    passes = key_passes(it)
+                    for kp in range(passes):
+                        block = (j // 2) * passes + kp
+                        nc.tensor.matmul_mx(
+                            out=att[group][:, j, :],
+                            lhsT=sc_codes[group, n % 2][:, block, :].bitcast(FP8X4),
+                            lhsT_scale=sc_scales[group, n % 2][:, block, :],
+                            rhs=v_codes[b][:, kp, :].bitcast(FP8X4),
+                            rhs_scale=v_scales[b][:, kp, :],
+                            start=(kp == 0),
+                            stop=(kp == passes - 1),
+                        )
+
+        def square_sums(s):
+            for group in group_due(s, 7):
+                squares = stage.tile([P, GROUP, HD], F32, name="squares")
+                sum_sq[group] = stat.tile([P, GROUP], F32, name="sum_sq")
+                for j in range(GROUP):
+                    nc.scalar.activation(
+                        out=squares[:, j, :],
+                        in_=att[group][:, j, :],
+                        func=ACT.Square,
+                        accum_out=sum_sq[group][:, j : j + 1],
+                    )
+
+        def row_rms(s):
+            for group in group_due(s, 7):
+                mean_sq = stat.tile([P, GROUP], F32, name="mean_sq")
+                nc.gpsimd.tensor_scalar(
+                    out=mean_sq[:], in0=sum_sq[group][:], scalar1=1.0 / HD, scalar2=EPS, op0=ALU.mult, op1=ALU.add
                 )
+                rstd[group] = stat.tile([P, GROUP], F32, name="rstd")
+                nc.gpsimd.tensor_tensor(out=rstd[group][:], in0=mean_sq[:], in1=neg_half[:], op=ALU.pow)
 
-        def row_rms(group):
-            mean_sq = stat.tile([P, GROUP], F32, name="mean_sq")
-            nc.gpsimd.tensor_scalar(
-                out=mean_sq[:], in0=sum_sq[group][:], scalar1=1.0 / HD, scalar2=EPS, op0=ALU.mult, op1=ALU.add
-            )
-            rstd[group] = stat.tile([P, GROUP], F32, name="rstd")
-            nc.gpsimd.tensor_tensor(out=rstd[group][:], in0=mean_sq[:], in1=neg_half[:], op=ALU.pow)
+        def finish(s):
+            for group in group_due(s, 8):
+                result = stage.tile([P, GROUP, HD], F32, name="result")
+                for j in range(GROUP):
+                    nc.vector.scalar_tensor_tensor(
+                        out=result[:, j, :],
+                        in0=att[group][:, j, :],
+                        scalar=rstd[group][:, j : j + 1],
+                        in1=gain[:],
+                        op0=ALU.mult,
+                        op1=ALU.mult,
+                    )
+                    b, it = locate(group * GROUP + j)
+                    nc.sync.dma_start(out=out[b, it * P : (it + 1) * P, 0, :], in_=result[:, j, :])
 
-        def finish(group):
-            result = stage.tile([P, GROUP, HD], F32, name="result")
-            for j in range(GROUP):
-                nc.vector.scalar_tensor_tensor(
-                    out=result[:, j, :],
-                    in0=att[group][:, j, :],
-                    scalar=rstd[group][:, j : j + 1],
-                    in1=gain[:],
-                    op0=ALU.mult,
-                    op1=ALU.mult,
-                )
-                b, it = where(group * GROUP + j)
-                nc.sync.dma_start(out=out[b, it * P : (it + 1) * P, 0, :], in_=result[:, j, :])
+        def run_step(s):
+            max_narrow(s)
+            max_wide(s)
+            energies_of_wide(s, 1)
+            exp_narrow(s)
+            copy_sc_wide(s)
+            exp_wide(s, 1)
+            next_rounded(s, 1)
+            energies_of_wide(s, 0)
+            next_rounded(s, 0)
+            copy_sc_narrow(s)
+            finish(s)
+            exp_wide(s, 0)
+            for i in range(PAIR):
+                transpose_h(s, i)
+            next_narrow(s, 1)
+            transpose_qk(s)
+            next_narrow(s, 0)
+            for i in range(PAIR):
+                copy_h(s, i)
+            copy_qk(s)
+            project_v(s)
+            attend(s)
+            next_wide(s)
+            copy_v(s)
+            square_sums(s)
+            combine(s)
+            transpose_sc(s)
+            quantise_h(s)
+            quantise_v(s)
+            quantise_sc(s)
+            invert_sums(s)
+            weigh_second(s)
+            add_part_sums(s)
+            row_rms(s)
 
-        STEPS = ITEMS // 2
-        PIECES = 4 * B
+        def run_last_step(s):
+            max_narrow(s)
+            max_wide(s)
+            exp_narrow(s)
+            exp_wide(s, 1)
+            exp_wide(s, 0)
+            invert_sums(s)
+            weigh_second(s)
+            copy_sc_wide(s)
+            copy_sc_narrow(s)
+            finish(s)
+            for i in range(PAIR):
+                transpose_h(s, i)
+            for i in range(PAIR):
+                copy_h(s, i)
+            project_v(s)
+            attend(s)
+            copy_v(s)
+            square_sums(s)
+            row_rms(s)
+            combine(s)
+            transpose_sc(s)
+            quantise_v(s)
+            quantise_h(s)
+            quantise_sc(s)
 
-        def lead(n):
-            for c in (1, 0):
-                pass
-
-        def look(s, kind, c):
-            n = 2 * s + kind
-            if 0 <= s < STEPS:
-                if is_direct(n):
-                    rounded_energies(n, c)
-                else:
-                    energies(n, c)
-
-        def h_step(m):
-            return max(m // 3, m // 2 - H_LEAD)
-
-        def stages(s):
-            a, w = 2 * s, 2 * s + 1
-            live = 0 <= s < STEPS
-            direct = live and is_direct(w)
-            st = {}
-            spare = nc.vector.tensor_copy if s < HEAD else nc.scalar.copy
-
-            def add(name, ok, *calls):
-                st[name] = calls if ok else ()
-
-            add("Ma", live, (scale_and_max, a, (1, 0)))
-            if direct:
-                add("Mw1", live, (row_max, w, 1))
-                add("Mw0", live, (row_max, w, 0))
-            else:
-                add("Mw1", live, (scale_and_max, w, (1, 0)))
-                add("Mw0", False)
-            add("Ew1", direct, (energies, w, 1))
-            add("Ew0a", direct, (energies, w, 0, slice(0, 1)))
-            add("Ew0b", direct, (energies, w, 0, slice(1, 2)))
-            add("Xa1", live, (exponentials, a, 1))
-            add("Xa0", live, (exponentials, a, 0))
-            add("Xw1", live, (exponentials, w, 1))
-            add("Xw0", live, (exponentials, w, 0))
-            add("PS", direct, (add_part_sums, s))
-            add("La1", True, (look, s + 1, 0, 1))
-            add("La0", True, (look, s + 1, 0, 0))
-            ahead = s + 1 < STEPS and is_direct(w + 2)
-            add("Lw1", ahead, (look, s + 1, 1, 1))
-            add("Lw0", ahead, (look, s + 1, 1, 0))
-            add("Ly", not ahead, (look, s + 1, 1, 1), (look, s + 1, 1, 0))
-            hm = [m for m in range(B * TILES) if h_step(m) == s]
-            for i in range(2):
-                mine = [m for m in hm if m % 2 == i]
-                add("H%dt" % i, live and mine, *[(transpose_h, m) for m in mine])
-                add("H%dc" % i, live and mine, *[(copy_h, m, spare) for m in mine])
-            qh = [p for p in range(ITEMS // 2) if h_step(2 * p + 1) + 1 == s]
-            add("QH", qh, *[(quantise_h, p) for p in qh])
-            pieces = [p for p in range(4, PIECES) if 4 * (p // 4 - 1) + QK_AT[p % 4] == s]
-            add("QKt", True, *[(transpose_qk, p) for p in pieces])
-            add("QKc", True, *[(copy_qk, p, spare) for p in pieces])
-            vg = [g for g in range(2 * B) if h_step(4 * g + 2) + V_AFTER == s]
-            add("Vt", vg, *[(project_v, g) for g in vg])
-            add("Vc", vg, *[(copy_v, g) for g in vg])
-            vq = [g for g in range(2 * B) if h_step(4 * g + 2) + V_AFTER + QV_AFTER == s]
-            add("QV", vq, *[(quantise_v, g) for g in vq])
-            def due(lag, limit=STEPS + 8):
-                return [t for t in range(STEPS) if min(t + lag, limit) == s]
-
-            def due_pairs(lag, limit=STEPS + 8):
-                return [t for t in due(lag, limit) if t % 2 == 1]
-
-            ts = due(R_LAG)
-            add("R", ts, *[(invert_sums, t) for t in ts])
-            add("W", ts, *[(weigh_second, n, nc.gpsimd if t < STEPS - 2 else nc.vector) for t in ts for n in (2 * t, 2 * t + 1)])
-            ts = due(CB_LAG, CB_END)
-            add("CBa", ts, *[(combine, 2 * t) for t in ts])
-            add("CBw", ts, *[(combine, 2 * t + 1) for t in ts])
-            add("Tw", ts, *[(transpose_sc, [2 * t + 1], 2 * t + 1) for t in ts])
-            add("Ta", ts, *[(transpose_sc, [2 * t - 2, 2 * t], 2 * t) for t in ts if t % 2 == 1])
-            ts = due(CS_LAG, CS_END)
-            late = nc.scalar.copy if s >= STEPS - 1 else nc.vector.tensor_copy
-            add("CSw", ts, *[(copy_sc, 2 * t + 1, t // 2, 2 * (t % 2), nc.scalar.copy if where(2 * t + 1)[1] in SC_ON_SCALAR else late) for t in ts])
-            add("CSa", ts, *[(copy_sc, 2 * t, t // 2, 0, nc.scalar.copy if t % 4 == 3 else late) for t in ts if t % 2 == 1])
-            ts = due_pairs(QS_LAG, CS_END)
-            add("QSw", ts, *[(quantise_sc, t // 2, 1) for t in ts])
-            add("QSa", ts, *[(quantise_sc, t // 2, 0) for t in ts])
-            ts = due_pairs(ATT_LAG, ATT_END)
-            add("At", ts, *[(attend, t // 2) for t in ts])
-            add("Sq", ts, *[(square_sums, t // 2) for t in ts])
-            add("RR", ts, *[(row_rms, t // 2) for t in ts])
-            ts = due_pairs(F_LAG, ATT_END + 1)
-            add("F", ts, *[(finish, t // 2) for t in ts])
-            return st
-
-        for piece in range(4):
-            transpose_qk(piece)
-            copy_qk(piece, nc.vector.tensor_copy if piece % 2 else nc.scalar.copy)
-        for kind in (0, 1):
-            for c in (1, 0):
-                look(0, kind, c)
+        for i in range(4):
+            transpose_piece(0, i)
+            copy_piece(0, i, nc.vector.tensor_copy if i % 2 else nc.scalar.copy)
+        next_narrow(-1, 1)
+        next_narrow(-1, 0)
+        next_rounded(-1, 1)
+        next_rounded(-1, 0)
         load_h(0)
         load_qk(1)
         for s in range(STEPS + 8):
-            b, j = divmod(s, 4)
+            b, j = divmod(s, BATCH_STEPS)
             if j == 0 and b + 1 < B:
                 if b + 2 < B:
                     load_qk(b + 2)
                 load_h(b + 1)
-            st = stages(s)
-            for name in (ORDER if s < STEPS - 1 else TAIL_ORDER).split():
-                for call in st[name]:
-                    call[0](*call[1:])
+            if s < STEPS - 1:
+                run_step(s)
+            else:
+                run_last_step(s)
             if s == 0:
-                copy_words(transpose_words(wv_raw[:]), wv_grouped[:], nc.scalar.copy)
+                copy_words(transpose_words(wv_raw[:]), wv_grouped[:])
             if s == 1:
                 quantise_wv()

import math
from contextlib import ExitStack

import concourse.mybir as mybir
from concourse.masks import make_identity

F32 = mybir.dt.float32
BF16 = mybir.dt.bfloat16
U32 = mybir.dt.uint32
U8 = mybir.dt.uint8
FP8X4 = mybir.dt.float8_e4m3fn_x4
ALU = mybir.AluOpType
ACT = mybir.ActivationFunctionType
AXIS = mybir.AxisListType

B, S, D, HD, C = 8, 1024, 1024, 128, 2
EPS = 1e-9
P = 128
TILES = S // P
BANK = 512
K_PASS = 512
ITEMS = B * TILES
STEPS = ITEMS // 2
BATCH_STEPS = TILES // 2
GROUP = 4
PAIR = 2
FROM_PSUM = 5
SM_SCALE = 1.0 / math.sqrt(HD)
LOG2_E = 1.0 / math.log(2.0)
MASKED = -1.0e30

FLOPS = 2 * B * S * D * HD + 2 * B * C * S * S * HD + 2 * B * S * S * HD


def key_passes(it):
    return (it * P) // K_PASS + 1


def narrow(step):
    return 2 * step


def wide(step):
    return 2 * step + 1


def is_wide(n):
    return n % 2 == 1


def locate(n):
    b, i = divmod(n, TILES)
    return b, (TILES - 1 - i // 2 if is_wide(n) else i // 2)


def row_width(n):
    return (locate(n)[1] + 1) * P


def key_runs(n):
    return [(lo, min(BANK, row_width(n) - lo)) for lo in range(0, row_width(n), BANK)]


def from_psum(n):
    return locate(n)[1] >= FROM_PSUM


def due(step, lag):
    return [step - lag] if 0 <= step - lag < STEPS else []


def group_due(step, lag):
    return [t // 2 for t in due(step, lag) if t % 2 == 1]


def tile_attention_pb_t_kernel(
    tc, q_rot, k_rot, h_norm, wv, head_norm_w, q1, q2, k1, k2, lam_init, out
):
    nc = tc.nc
    with ExitStack() as ctx:
        ctx.enter_context(tc.manual_schedule())
        const = ctx.enter_context(tc.tile_pool(name="const", bufs=1))
        raw = ctx.enter_context(tc.tile_pool(name="raw", bufs=2))
        batch = ctx.enter_context(tc.tile_pool(name="batch", bufs=2))
        stage = ctx.enter_context(tc.tile_pool(name="stage", bufs=3))
        soft = ctx.enter_context(tc.tile_pool(name="soft", bufs=2))
        expos = ctx.enter_context(tc.tile_pool(name="expos", bufs=3))
        stat = ctx.enter_context(tc.tile_pool(name="stat", bufs=4))
        codes = ctx.enter_context(tc.tile_pool(name="codes", bufs=3))
        psum_e = ctx.enter_context(tc.psum_pool(name="psum_e", bufs=3))
        psum_r = ctx.enter_context(tc.psum_pool(name="psum_r", bufs=2))
        psum_in = ctx.enter_context(tc.psum_pool(name="psum_in", bufs=3))

        q_raw, k_raw, q_t, k_t, qk_bank = {}, {}, {}, {}, {}
        h_raw, h_bank, h_grouped, h_codes, h_scales = {}, {}, {}, {}, {}
        v_bank, v_grouped, v_codes, v_scales = {}, {}, {}, {}
        energy, rounded, neg_max, y, expo, part_sums, sums, inv = {}, {}, {}, {}, {}, {}, {}, {}
        sc_bank, sc_grouped, sc_codes, sc_scales = {}, {}, {}, {}
        att, sum_sq, rstd = {}, {}, {}

        def load_h(b):
            h_raw[b] = raw.tile([P, 2, 4 * D], BF16, name="h_raw")
            h_view = h_norm[b].rearrange("(g p t) k -> p g (t k)", p=P, t=4)
            for g in range(2):
                for half in range(2):
                    cols = slice(half * 2 * D, (half + 1) * 2 * D)
                    nc.sync.dma_start(out=h_raw[b][:, g, cols], in_=h_view[:, g, cols])

        def load_qk(b):
            q_raw[b] = raw.tile([P, TILES, C * HD], BF16, name="q_raw")
            k_raw[b] = raw.tile([P, TILES, C * HD], BF16, name="k_raw")
            parts = 2 if b == 0 else 1
            for i in range(parts):
                tiles = slice(i * TILES // parts, (i + 1) * TILES // parts)
                tokens = slice(i * S // parts, (i + 1) * S // parts)
                for dst, src in ((q_raw[b], q_rot), (k_raw[b], k_rot)):
                    nc.sync.dma_start(
                        out=dst[:, tiles, :], in_=src[b, tokens, 0, :].rearrange("(t p) d -> p t d", p=P)
                    )

        rows = const.tile([P, 6 * P], BF16, name="rows")
        nc.vector.memset(rows[:], 0.0)
        for i, vec in enumerate((q1, q2, k1, k2)):
            nc.scalar.dma_start(out=rows[0:1, i * P : (i + 1) * P], in_=vec.rearrange("h d o -> h (d o)"))
        nc.scalar.dma_start(out=rows[0:1, 4 * P : 5 * P], in_=head_norm_w.rearrange("(o d) -> o d", o=1))
        nc.scalar.dma_start(out=rows[0:1, 5 * P : 5 * P + 1], in_=lam_init.rearrange("(o d) -> o d", o=1))
        first_exp = const.tile([P, 1], F32, name="first_exp")
        nc.vector.memset(first_exp[:], 0.0)
        nc.scalar.activation(out=first_exp[:], in_=first_exp[:], func=ACT.Exp)
        load_qk(0)
        wv_raw = const.tile([P, D], BF16, name="wv_raw")
        nc.sync.dma_start(out=wv_raw[:], in_=wv)

        ones_bf = const.tile([P, P], BF16, name="ones_bf")
        nc.vector.memset(ones_bf[:], 1.0)
        two = const.tile([P, 2], F32, name="two")
        nc.vector.memset(two[:], 2.0)
        ident_bf = const.tile([P, P], BF16, name="ident_bf")
        make_identity(nc, ident_bf[:])
        mask_f32 = const.tile([P, P], F32, name="mask_f32")
        nc.gpsimd.memset(mask_f32[:], 0.0)
        nc.gpsimd.affine_select(
            out=mask_f32[:],
            in_=mask_f32[:],
            compare_op=ALU.is_ge,
            fill=MASKED,
            base=0,
            pattern=[[-1, P]],
            channel_multiplier=1,
        )
        mask_bf = const.tile([P, P], BF16, name="mask_bf")
        nc.vector.tensor_copy(out=mask_bf[:], in_=mask_f32[:])
        ident_f32 = const.tile([P, P], F32, name="ident_f32")
        make_identity(nc, ident_f32[:])
        neg_half = const.tile([P, GROUP], F32, name="neg_half")
        nc.gpsimd.memset(neg_half[:], -0.5)

        sc_rows = []
        for it in range(TILES):
            sc_tile = const.tile([P, key_passes(it) * K_PASS], BF16, name="sc_rows%d" % it)
            if (it + 1) * P < key_passes(it) * K_PASS:
                nc.vector.memset(sc_tile[:, (it + 1) * P :], 0.0)
            sc_rows.append(sc_tile)

        spread = const.tile([P, 6 * P], F32, name="spread")
        bank_a = psum_in.tile([P, 4 * P], F32, name="bank_a", tag="tin")
        nc.tensor.matmul(bank_a[:], lhsT=ones_bf[:], rhs=rows[:, : 4 * P], start=True, stop=True)
        nc.vector.tensor_copy(out=spread[:, : 4 * P], in_=bank_a[:])
        bank_b = psum_in.tile([P, 2 * P], F32, name="bank_b", tag="tin")
        nc.tensor.matmul(bank_b[:], lhsT=ones_bf[:], rhs=rows[:, 4 * P :], start=True, stop=True)
        nc.vector.tensor_copy(out=spread[:, 4 * P :], in_=bank_b[:])
        lam = spread[:, 5 * P : 5 * P + 1]
        products = const.tile([P, 2, P], F32, name="products")
        nc.vector.tensor_tensor(
            out=products[:].rearrange("p a d -> p (a d)"),
            in0=spread[:, : 2 * P],
            in1=spread[:, 2 * P : 4 * P],
            op=ALU.mult,
        )
        one_minus_lam = const.tile([P, 1], F32, name="one_minus_lam")
        nc.vector.tensor_scalar(
            out=one_minus_lam[:], in0=lam, scalar1=-1.0, scalar2=1.0, op0=ALU.mult, op1=ALU.add
        )
        dots = const.tile([P, 2], F32, name="dots")
        nc.vector.tensor_reduce(out=dots[:], in_=products[:], axis=AXIS.X, op=ALU.add)
        gain = const.tile([P, HD], F32, name="gain")
        nc.vector.tensor_scalar(
            out=gain[:], in0=spread[:, 4 * P : 5 * P], scalar1=one_minus_lam[:], scalar2=None, op0=ALU.mult
        )
        log2_exp = const.tile([P, 2], F32, name="log2_exp")
        nc.vector.tensor_scalar(out=log2_exp[:], in0=dots[:], scalar1=LOG2_E, scalar2=None, op0=ALU.mult)
        exp_dots = const.tile([P, 2], F32, name="exp_dots")
        nc.gpsimd.tensor_tensor(out=exp_dots[:], in0=two[:], in1=log2_exp[:], op=ALU.pow)
        scale = const.tile([P, 1], F32, name="scale")
        nc.gpsimd.tensor_tensor(out=scale[:], in0=exp_dots[:, 1:2], in1=exp_dots[:, 0:1], op=ALU.subtract)
        nc.gpsimd.tensor_tensor(out=scale[:], in0=scale[:], in1=lam, op=ALU.subtract)

        def transpose_words(src_bf16):
            words = src_bf16.bitcast(F32)
            bank = psum_in.tile([P, 4, P], F32, name="word_bank", tag="tin")
            for w in range(4):
                nc.tensor.transpose(bank[:, w, :], words[:, w * P : (w + 1) * P], ident_f32[:])
            return bank

        def copy_words(bank, grouped):
            nc.scalar.copy(out=grouped.bitcast(F32), in_=bank[:].rearrange("p (g u) r -> p g r u", u=2))

        wv_grouped = const.tile([P, 2, P, 4], BF16, name="wv_grouped", align_bytes=64)
        wv_codes = const.tile([P, 2, P], U32, name="wv_codes", align_bytes=64)
        wv_scales = const.tile([P, 2, P], U8, name="wv_scales", align_bytes=64)

        def quantise_wv():
            nc.vector.quantize_mx(
                out=wv_codes[:].rearrange("p g r -> p (g r)").bitcast(FP8X4),
                scales=wv_scales[:].rearrange("p g r -> p (g r)"),
                in_=wv_grouped[:].rearrange("p g r t -> p (g r t)"),
            )

        def transpose_h(s, i):
            for t in due(s, 0):
                b, st = divmod(PAIR * t + i, TILES)
                g, slot = divmod(st, 4)
                if i == 0:
                    h_grouped[t] = stage.tile([P, PAIR, 2, P, 4], BF16, name="h_grouped", align_bytes=64)
                h_bank[t, i] = transpose_words(h_raw[b][:, g, slot * D : (slot + 1) * D])

        def copy_h(s, i):
            for t in due(s, 0):
                copy_words(h_bank[t, i], h_grouped[t][:, i])

        def quantise_h(s):
            for t in due(s, 1):
                b, st = divmod(PAIR * t, TILES)
                if st == 0:
                    h_codes[b] = batch.tile([P, TILES, 2, P], U32, name="h_codes", align_bytes=64)
                    h_scales[b] = batch.tile([P, TILES, 2, P], U8, name="h_scales", align_bytes=64)
                nc.vector.quantize_mx(
                    out=h_codes[b][:, st : st + PAIR].rearrange("p i g r -> p (i g r)").bitcast(FP8X4),
                    scales=h_scales[b][:, st : st + PAIR].rearrange("p i g r -> p (i g r)"),
                    in_=h_grouped[t][:].rearrange("p i g r t -> p (i g r t)"),
                )

        def project_v(s):
            for vg in group_due(s, 2):
                b, kp = divmod(vg, 2)
                v_bank[vg] = psum_in.tile([P, 4, HD], F32, name="v_bank", tag="tin")
                for t in range(4):
                    st = 4 * kp + t
                    for g in range(2):
                        nc.tensor.matmul_mx(
                            out=v_bank[vg][:, t, :],
                            lhsT=h_codes[b][:, st, g, :].bitcast(FP8X4),
                            lhsT_scale=h_scales[b][:, st, g, :],
                            rhs=wv_codes[:, g, :].bitcast(FP8X4),
                            rhs_scale=wv_scales[:, g, :],
                            start=(g == 0),
                            stop=(g == 1),
                        )

        def copy_v(s):
            for vg in group_due(s, 2):
                v_grouped[vg] = stage.tile([P, HD, 4], BF16, name="v_grouped", align_bytes=64)
                nc.scalar.copy(out=v_grouped[vg][:], in_=v_bank[vg][:].rearrange("p t d -> p d t"))

        def quantise_v(s):
            for vg in group_due(s, 3):
                b, kp = divmod(vg, 2)
                if kp == 0:
                    v_codes[b] = batch.tile([P, 2, HD], U32, name="v_codes", align_bytes=64)
                    v_scales[b] = batch.tile([P, 2, HD], U8, name="v_scales", align_bytes=64)
                nc.vector.quantize_mx(
                    out=v_codes[b][:, kp, :].bitcast(FP8X4),
                    scales=v_scales[b][:, kp, :],
                    in_=v_grouped[vg][:].rearrange("p d t -> p (d t)"),
                )

        def transpose_piece(b, i):
            c, is_k = 1 - i // 2, i % 2
            if i == 0:
                q_t[b] = batch.tile([P, C, S], BF16, name="q_t")
                k_t[b] = batch.tile([P, C, S], BF16, name="k_t")
            src = k_raw[b] if is_k else q_raw[b]
            qk_bank[b, i] = psum_in.tile([P, TILES, P], BF16, name="qk_bank", tag="tin")
            for t in range(TILES):
                nc.tensor.transpose(qk_bank[b, i][:, t, :], src[:, t, c * HD : (c + 1) * HD], ident_bf[:])

        def copy_piece(b, i, copy_out):
            c, is_k = 1 - i // 2, i % 2
            dst = k_t[b] if is_k else q_t[b]
            copy_out(out=dst[:, c, :], in_=qk_bank[b, i][:].rearrange("p t r -> p (t r)"))

        def pieces_due(s):
            b, j = divmod(s, BATCH_STEPS)
            return [(b + 1, i) for i in range(4) if max(0, i - 1) == j and b + 1 < B]

        def transpose_qk(s):
            for b, i in pieces_due(s):
                transpose_piece(b, i)

        def copy_qk(s):
            for b, i in pieces_due(s):
                copy_piece(b, i, nc.scalar.copy)

        def multiply_qk(n, c, lo, cols, dst):
            b, it = locate(n)
            has_diagonal = lo + cols == row_width(n)
            nc.tensor.matmul(
                dst,
                lhsT=q_t[b][:, c, it * P : (it + 1) * P],
                rhs=k_t[b][:, c, lo : lo + cols],
                start=True,
                stop=not has_diagonal,
            )
            if has_diagonal:
                nc.tensor.matmul(dst[:, cols - P :], lhsT=ident_bf[:], rhs=mask_bf[:], start=False, stop=True)

        def energies(n, c):
            for lo, cols in key_runs(n):
                bank = psum_e.tile([P, BANK], F32, name="energy")
                energy[n, c, lo] = bank[:, :cols]
                multiply_qk(n, c, lo, cols, energy[n, c, lo])

        def rounded_energies(n, c):
            rounded[n, c] = psum_r.tile([P, S], BF16, name="rounded")
            for lo, cols in key_runs(n):
                multiply_qk(n, c, lo, cols, rounded[n, c][:, lo : lo + cols])

        def energies_of_wide(s, c):
            for t in due(s, 0):
                if from_psum(wide(t)):
                    energies(wide(t), c)

        def next_narrow(s, c):
            for t in due(s + 1, 0):
                energies(narrow(t), c)

        def next_rounded(s, c):
            for t in due(s + 1, 0):
                if from_psum(wide(t)):
                    rounded_energies(wide(t), c)

        def next_wide(s):
            for t in due(s + 1, 0):
                if not from_psum(wide(t)):
                    for c in (1, 0):
                        energies(wide(t), c)

        def scale_and_max(n):
            for c in (1, 0):
                y[n, c] = soft.tile([P, FROM_PSUM * P], F32, name="y%d" % c)
            for lo, cols in key_runs(n):
                for c in (1, 0):
                    so_far = neg_max[n, c][:] if lo > 0 else None
                    neg_max[n, c] = stat.tile([P, 1], F32, name="neg_max%d" % c)
                    nc.vector.tensor_scalar(
                        out=y[n, c][:, lo : lo + cols],
                        in0=energy[n, c, lo],
                        scalar1=-SM_SCALE,
                        scalar2=so_far,
                        op0=ALU.mult,
                        op1=ALU.min,
                        accum_out=neg_max[n, c][:],
                    )

        def row_max(n, c):
            neg_max[n, c] = stat.tile([P, 1], F32, name="neg_max%d" % c)
            unused = soft.tile([P, S], BF16, name="unused")
            nc.vector.tensor_scalar(
                out=unused[:, : row_width(n)],
                in0=rounded[n, c][:, : row_width(n)],
                scalar1=-SM_SCALE,
                scalar2=None,
                op0=ALU.mult,
                op1=ALU.min,
                accum_out=neg_max[n, c][:],
            )

        def max_narrow(s):
            for t in due(s, 0):
                scale_and_max(narrow(t))

        def max_wide(s):
            for t in due(s, 0):
                if from_psum(wide(t)):
                    for c in (1, 0):
                        row_max(wide(t), c)
                else:
                    scale_and_max(wide(t))

        def exponentials(n, c):
            t = n // 2
            width = row_width(n)
            expo[n, c] = expos.tile(
                [P, S if is_wide(n) else BANK], F32, name="expo%d%d" % (1 if is_wide(n) else 0, c)
            )
            if t not in sums:
                sums[t] = stat.tile([P, 2, C], F32, name="sums")
            if from_psum(n):
                if t not in part_sums:
                    part_sums[t] = stat.tile([P, 2, C], F32, name="part_sums")
                for lo, cols in key_runs(n):
                    nc.scalar.activation(
                        out=expo[n, c][:, lo : lo + cols],
                        in_=energy[n, c, lo],
                        func=ACT.Exp,
                        bias=neg_max[n, c][:],
                        scale=SM_SCALE,
                        accum_out=part_sums[t][:, lo // BANK, c : c + 1],
                    )
            else:
                nc.scalar.activation(
                    out=expo[n, c][:, :width],
                    in_=y[n, c][:, :width],
                    func=ACT.Exp,
                    bias=neg_max[n, c][:],
                    scale=-1.0,
                    accum_out=sums[t][:, n % 2, c : c + 1],
                )

        def exp_narrow(s):
            for t in due(s, 0):
                for c in (1, 0):
                    exponentials(narrow(t), c)

        def exp_wide(s, c):
            for t in due(s, 0):
                exponentials(wide(t), c)

        def add_part_sums(s):
            for t in due(s, 0):
                if from_psum(wide(t)):
                    nc.gpsimd.tensor_tensor(
                        out=sums[t][:, 1, :], in0=part_sums[t][:, 0, :], in1=part_sums[t][:, 1, :], op=ALU.add
                    )

        def invert_sums(s):
            for t in due(s, 1):
                inv[t] = stat.tile([P, 2, C], F32, name="inv")
                nc.vector.reciprocal(
                    out=inv[t][:].rearrange("p i c -> p (i c)"), in_=sums[t][:].rearrange("p i c -> p (i c)")
                )

        def weigh_second(s):
            for t in due(s, 1):
                engine = nc.gpsimd if t < STEPS - 2 else nc.vector
                for n in (narrow(t), wide(t)):
                    engine.tensor_scalar(
                        out=expo[n, 1][:, : row_width(n)],
                        in0=expo[n, 1][:, : row_width(n)],
                        scalar1=inv[t][:, n % 2, 1:2],
                        scalar2=scale[:],
                        op0=ALU.mult,
                        op1=ALU.mult,
                    )

        def combine(s):
            for t in due(s, 2):
                for n in (wide(t), narrow(t)):
                    width = row_width(n)
                    nc.vector.scalar_tensor_tensor(
                        out=sc_rows[locate(n)[1]][:, :width],
                        in0=expo[n, 0][:, :width],
                        scalar=inv[t][:, n % 2, 0:1],
                        in1=expo[n, 1][:, :width],
                        op0=ALU.mult,
                        op1=ALU.add,
                    )

        def transpose_sc_of(items, key):
            sc_bank[key] = psum_in.tile([P, 4, P], F32, name="sc_bank", tag="tin")
            slot = 0
            for n in items:
                words = sc_rows[locate(n)[1]][:].bitcast(F32)
                for g in range(key_passes(locate(n)[1])):
                    for u in range(2):
                        nc.tensor.transpose(
                            sc_bank[key][:, slot, :], words[:, 2 * P * g + u : 2 * P * (g + 1) : 2], ident_f32[:]
                        )
                        slot += 1

        def transpose_sc(s):
            for t in due(s, 2):
                transpose_sc_of([wide(t)], wide(t))
                if t % 2 == 1:
                    transpose_sc_of([narrow(t - 1), narrow(t)], narrow(t))

        def copy_sc_of(key, first, blocks, copy_out):
            group = key // GROUP
            if first == 0:
                sc_grouped[group, key % 2] = stage.tile(
                    [P, blocks, P, 4], BF16, name="sc_grouped%d" % (key % 2), align_bytes=64
                )
            copy_out(
                out=sc_grouped[group, key % 2][:, first : first + 2].bitcast(F32),
                in_=sc_bank[key][:].rearrange("p (g u) r -> p g r u", u=2),
            )

        def copy_sc_wide(s):
            scalar_takes = s % BATCH_STEPS == 0 or s >= STEPS - 1
            for t in due(s, 3):
                copy_sc_of(wide(t), 2 * (t % 2), 4, nc.scalar.copy if scalar_takes else nc.vector.tensor_copy)

        def copy_sc_narrow(s):
            scalar_takes = s % BATCH_STEPS == 2 or s >= STEPS - 1
            for t in due(s, 3):
                if t % 2 == 1:
                    copy_sc_of(narrow(t), 0, 2, nc.scalar.copy if scalar_takes else nc.vector.tensor_copy)

        def quantise_sc(s):
            for group in group_due(s, 3):
                for kind, blocks in ((1, 4), (0, 2)):
                    sc_codes[group, kind] = codes.tile([P, blocks, P], U32, name="sc_codes%d" % kind, align_bytes=64)
                    sc_scales[group, kind] = codes.tile([P, blocks, P], U8, name="sc_scales%d" % kind, align_bytes=64)
                    nc.vector.quantize_mx(
                        out=sc_codes[group, kind][:].rearrange("p g r -> p (g r)").bitcast(FP8X4),
                        scales=sc_scales[group, kind][:].rearrange("p g r -> p (g r)"),
                        in_=sc_grouped[group, kind][:].rearrange("p g r t -> p (g r t)"),
                    )

        def attend(s):
            for group in group_due(s, 7):
                att[group] = psum_in.tile([P, GROUP, HD], F32, name="att", tag="tin")
                for j in range(GROUP):
                    n = group * GROUP + j
                    b, it = locate(n)
                    passes = key_passes(it)
                    for kp in range(passes):
                        block = (j // 2) * passes + kp
                        nc.tensor.matmul_mx(
                            out=att[group][:, j, :],
                            lhsT=sc_codes[group, n % 2][:, block, :].bitcast(FP8X4),
                            lhsT_scale=sc_scales[group, n % 2][:, block, :],
                            rhs=v_codes[b][:, kp, :].bitcast(FP8X4),
                            rhs_scale=v_scales[b][:, kp, :],
                            start=(kp == 0),
                            stop=(kp == passes - 1),
                        )

        def square_sums(s):
            for group in group_due(s, 7):
                squares = stage.tile([P, GROUP, HD], F32, name="squares")
                sum_sq[group] = stat.tile([P, GROUP], F32, name="sum_sq")
                for j in range(GROUP):
                    nc.scalar.activation(
                        out=squares[:, j, :],
                        in_=att[group][:, j, :],
                        func=ACT.Square,
                        accum_out=sum_sq[group][:, j : j + 1],
                    )

        def row_rms(s):
            for group in group_due(s, 7):
                mean_sq = stat.tile([P, GROUP], F32, name="mean_sq")
                nc.gpsimd.tensor_scalar(
                    out=mean_sq[:], in0=sum_sq[group][:], scalar1=1.0 / HD, scalar2=EPS, op0=ALU.mult, op1=ALU.add
                )
                rstd[group] = stat.tile([P, GROUP], F32, name="rstd")
                nc.gpsimd.tensor_tensor(out=rstd[group][:], in0=mean_sq[:], in1=neg_half[:], op=ALU.pow)

        def finish(s):
            for group in group_due(s, 8):
                result = stage.tile([P, GROUP, HD], F32, name="result")
                for j in range(GROUP):
                    nc.vector.scalar_tensor_tensor(
                        out=result[:, j, :],
                        in0=att[group][:, j, :],
                        scalar=rstd[group][:, j : j + 1],
                        in1=gain[:],
                        op0=ALU.mult,
                        op1=ALU.mult,
                    )
                    b, it = locate(group * GROUP + j)
                    nc.sync.dma_start(out=out[b, it * P : (it + 1) * P, 0, :], in_=result[:, j, :])

        def run_step(s):
            max_narrow(s)
            max_wide(s)
            energies_of_wide(s, 1)
            exp_narrow(s)
            copy_sc_wide(s)
            exp_wide(s, 1)
            next_rounded(s, 1)
            energies_of_wide(s, 0)
            next_rounded(s, 0)
            copy_sc_narrow(s)
            finish(s)
            exp_wide(s, 0)
            for i in range(PAIR):
                transpose_h(s, i)
            next_narrow(s, 1)
            transpose_qk(s)
            next_narrow(s, 0)
            for i in range(PAIR):
                copy_h(s, i)
            copy_qk(s)
            project_v(s)
            attend(s)
            next_wide(s)
            copy_v(s)
            square_sums(s)
            combine(s)
            transpose_sc(s)
            quantise_h(s)
            quantise_v(s)
            quantise_sc(s)
            invert_sums(s)
            weigh_second(s)
            add_part_sums(s)
            row_rms(s)

        def run_last_step(s):
            max_narrow(s)
            max_wide(s)
            exp_narrow(s)
            exp_wide(s, 1)
            exp_wide(s, 0)
            invert_sums(s)
            weigh_second(s)
            copy_sc_wide(s)
            copy_sc_narrow(s)
            finish(s)
            for i in range(PAIR):
                transpose_h(s, i)
            for i in range(PAIR):
                copy_h(s, i)
            project_v(s)
            attend(s)
            copy_v(s)
            square_sums(s)
            row_rms(s)
            combine(s)
            transpose_sc(s)
            quantise_v(s)
            quantise_h(s)
            quantise_sc(s)

        for i in range(4):
            transpose_piece(0, i)
            copy_piece(0, i, nc.vector.tensor_copy if i % 2 else nc.scalar.copy)
        next_narrow(-1, 1)
        next_narrow(-1, 0)
        next_rounded(-1, 1)
        next_rounded(-1, 0)
        load_h(0)
        load_qk(1)
        for s in range(STEPS + 8):
            b, j = divmod(s, BATCH_STEPS)
            if j == 0 and b + 1 < B:
                if b + 2 < B:
                    load_qk(b + 2)
                load_h(b + 1)
            if s < STEPS - 1:
                run_step(s)
            else:
                run_last_step(s)
            if s == 0:
                copy_words(transpose_words(wv_raw[:]), wv_grouped[:])
            if s == 1:
                quantise_wv()
